import numpy as np
import ml_dtypes


def mxq(x, axis, fmt="e4m3"):
    dtype, down = {"e4m3": (ml_dtypes.float8_e4m3fn, 7), "e5m2": (ml_dtypes.float8_e5m2, 14)}[fmt]
    v = np.moveaxis(np.asarray(x, np.float32).astype(ml_dtypes.bfloat16).astype(np.float64), axis, -1)
    blocks = v.reshape(v.shape[:-1] + (-1, 32))
    amax = np.abs(blocks).max(-1, keepdims=True)
    byte = np.maximum(np.where(amax > 0, np.frexp(amax)[1] - 1 + 127, 0) - down, 1)
    scale = np.exp2(byte - 127.0)
    codes = (blocks / scale).astype(np.float32).astype(dtype).astype(np.float64)
    return np.moveaxis((codes * scale).reshape(v.shape), -1, axis)


WIDE = False


def mx_kscale(k):
    if not WIDE:
        return np.ones(k)
    levels = np.array([10, -10, 5, -5, 0])
    if k % 512:
        return np.exp2(np.random.permutation(np.resize(levels, k // 32))).repeat(32)
    a = np.empty((k // 512, 16))
    for p in range(k // 512):
        a[p, :8] = np.random.permutation(np.resize(levels, 8))
        for g in range(8):
            far = levels[np.abs(levels - a[p, g]) >= 10]
            a[p, g + 8] = far[np.random.randint(len(far))]
    return np.exp2(a.ravel()).repeat(32)


BF16 = ml_dtypes.bfloat16


def bf(x):
    return np.asarray(x, np.float32).astype(BF16)


def f64(x):
    return np.asarray(x).astype(np.float64)


B, T, D, O = 512, 32, 512, 128


def erf(z):
    a = np.clip(z, -6.0, 6.0)
    q = 2.0 * a * a
    term = a.copy()
    total = a.copy()
    for k in range(1, 130):
        term = term * q / (2 * k + 1)
        total = total + term
    return 2.0 / np.sqrt(np.pi) * np.exp(-a * a) * total


def gelu_exact(v):
    return 0.5 * v * (1.0 + erf(v / np.sqrt(2.0)))


def setup_inputs():
    s = mx_kscale(D)
    x = np.random.standard_normal((B, T, D)) * s
    lengths = np.random.randint(T // 4, T + 1, size=B)
    lengths[np.random.randint(B)] = T
    pad = np.arange(T)[None, :] >= lengths[:, None]
    x = np.where(pad[:, :, None], -1.0, x)
    return {"x": bf(x), "W": bf(np.random.standard_normal((O, D)) / np.sqrt(D) / s[None, :]), "b": bf(np.random.standard_normal(O) * 0.3)}


def reference(x, W, b):
    x = f64(x)
    valid = ~np.all(x == -1.0, axis=-1)
    y = gelu_exact((mxq(x, 2, "e4m3") @ mxq(f64(W), 1, "e4m3").T) + f64(b))
    vf = valid[..., None].astype(np.float64)
    n = np.sum(vf, axis=1)
    mean = np.sum(y * vf, axis=1) / n
    diff = (y - mean[:, None, :]) * vf
    var = np.sum(diff * diff, axis=1) / np.maximum(n - 1.0, 1.0)
    std = np.where(n > 1.0, np.sqrt(var), np.zeros_like(var))
    out = np.concatenate([std, mean], axis=-1)
    return np.where(np.isnan(out), np.zeros_like(out), out)

@@ -1,0 +1,278 @@
+from contextlib import ExitStack
+
+import concourse.mybir as mybir
+from concourse.masks import make_identity
+
+F32 = mybir.dt.float32
+BF16 = mybir.dt.bfloat16
+U32 = mybir.dt.uint32
+U8 = mybir.dt.uint8
+FP8X4 = mybir.dt.float8_e4m3fn_x4
+ACT = mybir.ActivationFunctionType
+ALU = mybir.AluOpType
+AX = mybir.AxisListType
+
+P = 128
+B, T, D, O = 512, 32, 512, 128
+ROWS_PP = B * T // P
+SPP = ROWS_PP // T
+WORDS = D // 2
+UNIT = 4
+NU = ROWS_PP // UNIT
+UPS = T // UNIT
+FLOPS = 2 * B * T * D * O
+PAD_WORD = -(1.0 + 49024.0 / 8388608.0)
+CHUNKS = [4, 4, 4, 4] + [8] * 14
+
+LA_TEST, LA_DIAG, LA_XPOSE = 5, 3, 2
+LAG_QUANT, LAG_GELU, LAG_SQ_V, LAG_ACC = 1, 3, 4, 5
+TAIL_S = 3
+PER_SQ_V = 8
+
+
+def evac_on_scalar(h, pr):
+    return pr == 1 and h >= NU - TAIL_S
+
+
+def square_on_vector(h):
+    return h % PER_SQ_V == PER_SQ_V - 1 and h < NU - 2
+
+
+def tile_linearnnencoder_t_kernel(tc, x, W, b, out):
+    nc = tc.nc
+    xv = x.flatten_outer_dims().rearrange("(p r) k -> p r k", p=P)
+    ov = out.rearrange("(p j) c -> p j c", j=SPP)
+    with ExitStack() as ctx:
+        keep = ctx.enter_context(tc.tile_pool(name="keep", bufs=1))
+        jk = ctx.enter_context(tc.tile_pool(name="jk", bufs=2))
+        dgp = ctx.enter_context(tc.tile_pool(name="dgp", bufs=5))
+        gp = ctx.enter_context(tc.tile_pool(name="gp", bufs=4))
+        cp = ctx.enter_context(tc.tile_pool(name="cp", bufs=4))
+        ys = ctx.enter_context(tc.tile_pool(name="ys", bufs=6))
+        fs = ctx.enter_context(tc.tile_pool(name="fs", bufs=4))
+        fin = ctx.enter_context(tc.tile_pool(name="fin", bufs=2))
+        pacc = ctx.enter_context(tc.psum_pool(name="pacc", bufs=1))
+        pxt = ctx.enter_context(tc.psum_pool(name="pxt", bufs=4))
+        pmx = ctx.enter_context(tc.psum_pool(name="pmx", bufs=2))
+
+        w_sb = keep.tile([P, D], BF16)
+        nc.sync.dma_start(out=w_sb[:], in_=W)
+        zb = keep.tile([P, O], BF16)
+        nc.vector.memset(zb[:], 0.0)
+        where = {}
+        r0 = 0
+        for c, n_t in enumerate(CHUNKS):
+            xc = keep.tile([P, n_t, D], BF16, name="x%d" % c)
+            nc.sync.dma_start(out=xc[:], in_=xv[:, r0 : r0 + n_t, :])
+            for k in range(n_t):
+                where[r0 + k] = (xc, k)
+            r0 += n_t
+            if c == 0:
+                nc.sync.dma_start(out=zb[0:1, :], in_=b.rearrange("(u o) -> u o", u=1))
+
+        ident = keep.tile([P, P], F32)
+        make_identity(nc, ident[:])
+        negc = keep.tile([P, 1], F32)
+        nc.vector.memset(negc[:], -PAD_WORD)
+        ones = keep.tile([P, P], BF16)
+        nc.vector.memset(ones[:], 1.0)
+        warm = keep.tile([P, 1], F32)
+        nc.scalar.activation(out=warm[:], in_=negc[:], func=ACT.Gelu)
+
+        w_w = w_sb[:].bitcast(F32)
+        wt = pxt.tile([P, 2, 2, P], F32, tag="xt")
+        for u in range(2):
+            nc.tensor.transpose(wt[:, 0, u, :], w_w[:, u:WORDS:2], ident[:])
+        gw = keep.tile([P, O, 4], BF16, align_bytes=64)
+        nc.vector.tensor_copy(out=gw[:].bitcast(F32), in_=wt[:, 0, :, :].rearrange("q u o -> q o u"))
+        wc = keep.tile([P, O], U32, align_bytes=64)
+        wsc = keep.tile([P, O], U8, align_bytes=64)
+        nc.vector.quantize_mx(out=wc[:].bitcast(FP8X4), scales=wsc[:], in_=gw[:].rearrange("q o j -> q (o j)"))
+
+        bt = pxt.tile([P, 2, 2, P], F32, tag="xt")
+        nc.tensor.matmul(out=bt[:, 0, 0, :], lhsT=ones[:], rhs=zb[:], start=True, stop=True)
+        nc.tensor.matmul(out=bt[:, 1, 0, 0:64], lhsT=zb[:], rhs=ones[:, 0:64], start=True, stop=True)
+        bcol = keep.tile([P, 1], F32)
+        nc.vector.tensor_copy(out=bcol[:], in_=bt[:, 1, 0, 0:1])
+        c0 = keep.tile([P, O], F32)
+        c0sq = keep.tile([P, O], F32)
+
+        dev = keep.tile([P, NU, 8], F32)
+        vf = keep.tile([P, SPP, T], F32)
+        sm = keep.tile([P, SPP, 8], F32)
+        res = keep.tile([P, SPP, 2 * O], F32)
+        acc_y = pacc.tile([P, SPP, O], F32)
+        acc_q = pacc.tile([P, SPP, O], F32)
+        dg, xt, g, codes, sc, v, y, q, yf = {}, {}, {}, {}, {}, {}, {}, {}, {}
+        pre1, pre2 = {}, {}
+
+        def row_words(i):
+            xc, k = where[i]
+            return xc[:].bitcast(F32)[:, k, :]
+
+        def test(h):
+            for a in range(UNIT):
+                junk = jk.tile([P, WORDS], BF16, tag="junk")
+                nc.scalar.activation(
+                    out=junk[:],
+                    in_=row_words(h * UNIT + a),
+                    func=ACT.Square,
+                    bias=negc[:],
+                    scale=1.0,
+                    accum_out=dev[:, h, a : a + 1],
+                )
+
+        def diag(h):
+            dg[h] = dgp.tile([P, UNIT, P], F32, name="dg")
+            for a in range(UNIT):
+                nc.vector.tensor_scalar(
+                    out=dg[h][:, a, :],
+                    in0=ident[:],
+                    scalar1=dev[:, h, a : a + 1],
+                    scalar2=0.0,
+                    op0=ALU.mult,
+                    op1=ALU.is_gt,
+                )
+
+        def xpose(h):
+            for pr in range(2):
+                xt[h, pr] = pxt.tile([P, 2, 2, P], F32, name="xt")
+                for a in range(2):
+                    rw = row_words(h * UNIT + 2 * pr + a)
+                    for u in range(2):
+                        nc.tensor.transpose(xt[h, pr][:, a, u, :], rw[:, u:WORDS:2], dg[h][:, 2 * pr + a, :])
+
+        def evac(h):
+            g[h] = gp.tile([P, UNIT * P, 4], BF16, name="g", align_bytes=64)
+            g_w = g[h][:].bitcast(F32)
+            for pr in range(2):
+                dst = g_w[:, 2 * pr * P : (2 * pr + 2) * P, :].rearrange("q (a t) u -> q a t u", a=2)
+                src = xt[h, pr][:].rearrange("q a u t -> q a t u")
+                if evac_on_scalar(h, pr):
+                    nc.scalar.copy(out=dst, in_=src)
+                else:
+                    nc.vector.tensor_copy(out=dst, in_=src)
+
+        def quant(h):
+            codes[h] = cp.tile([P, UNIT * P], U32, name="codes", align_bytes=64)
+            sc[h] = cp.tile([P, UNIT * P], U8, name="sc", align_bytes=64)
+            nc.vector.quantize_mx(
+                out=codes[h][:].bitcast(FP8X4), scales=sc[h][:], in_=g[h][:].rearrange("q t j -> q (t j)")
+            )
+
+        def mx(h):
+            v[h] = pmx.tile([P, UNIT * P], F32, name="v")
+            nc.tensor.matmul_mx(
+                out=v[h][:],
+                lhsT=wc[:].bitcast(FP8X4),
+                lhsT_scale=wsc[:],
+                rhs=codes[h][:].bitcast(FP8X4),
+                rhs_scale=sc[h][:],
+                start=True,
+                stop=True,
+            )
+
+        def gelu(h):
+            y[h] = ys.tile([P, UNIT * P], F32, name="y")
+            nc.scalar.activation(out=y[h][:], in_=v[h][:], func=ACT.Gelu, bias=bcol[:], scale=1.0)
+
+        def square(h):
+            q[h] = ys.tile([P, UNIT * P], F32, name="q")
+            if square_on_vector(h):
+                nc.vector.tensor_tensor(out=q[h][:], in0=y[h][:], in1=y[h][:], op=ALU.mult)
+            else:
+                nc.scalar.activation(out=q[h][:], in_=y[h][:], func=ACT.Square)
+
+        def fold(h):
+            half = UNIT * P // 2
+            yf[h] = fs.tile([P, half], F32, name="yf")
+            nc.vector.tensor_tensor(out=yf[h][:], in0=y[h][:, 0:half], in1=y[h][:, half : 2 * half], op=ALU.add)
+
+        def accumulate(h):
+            j = h // UPS
+            for src, acc, n_t in ((yf, acc_y, UNIT // 2), (q, acc_q, UNIT)):
+                for a in range(n_t):
+                    nc.tensor.matmul(
+                        out=acc[:, j, :],
+                        lhsT=src[h][:, a * P : (a + 1) * P],
+                        rhs=ident[:],
+                        is_transpose=True,
+                        start=(h % UPS == 0 and a == 0),
+                        stop=(h % UPS == UPS - 1 and a == n_t - 1),
+                    )
+
+        def counts(j):
+            nc.vector.tensor_scalar(
+                out=vf[:, j, :].rearrange("p (h a) -> p h a", a=UNIT),
+                in0=dev[:, j * UPS : (j + 1) * UPS, 0:UNIT],
+                scalar1=0.0,
+                scalar2=None,
+                op0=ALU.is_gt,
+            )
+            n = sm[:, j, 0:1]
+            nc.vector.tensor_reduce(out=n, in_=vf[:, j, :], axis=AX.X, op=ALU.add)
+            nc.vector.tensor_scalar(out=sm[:, j, 1:2], in0=n, scalar1=-float(T), scalar2=None, op0=ALU.add)
+            nc.vector.tensor_scalar(out=sm[:, j, 2:3], in0=n, scalar1=1.0, scalar2=None, op0=ALU.max)
+            nc.vector.tensor_scalar(out=sm[:, j, 3:4], in0=n, scalar1=-1.0, scalar2=1.0, op0=ALU.add, op1=ALU.max)
+            nc.vector.reciprocal(out=sm[:, j, 4:6], in_=sm[:, j, 2:4])
+            nc.vector.scalar_tensor_tensor(
+                out=sm[:, j, 6:7], in0=n, scalar=0.0, in1=sm[:, j, 4:5], op0=ALU.is_gt, op1=ALU.mult
+            )
+            nc.vector.scalar_tensor_tensor(
+                out=sm[:, j, 7:8], in0=n, scalar=1.0, in1=sm[:, j, 5:6], op0=ALU.is_gt, op1=ALU.mult
+            )
+            pre1[j] = fin.tile([P, O], F32, name="pre1")
+            nc.vector.tensor_scalar(out=pre1[j][:], in0=c0[:], scalar1=sm[:, j, 1:2], scalar2=None, op0=ALU.mult)
+            pre2[j] = fin.tile([P, O], F32, name="pre2")
+            nc.vector.tensor_scalar(out=pre2[j][:], in0=c0sq[:], scalar1=sm[:, j, 1:2], scalar2=None, op0=ALU.mult)
+
+        def finish_mean(j):
+            s1 = fin.tile([P, O], F32, name="s1")
+            nc.vector.tensor_tensor(out=s1[:], in0=pre1[j][:], in1=acc_y[:, j, :], op=ALU.add)
+            nc.vector.tensor_scalar(
+                out=res[:, j, O : 2 * O], in0=s1[:], scalar1=sm[:, j, 6:7], scalar2=None, op0=ALU.mult
+            )
+            tt = fin.tile([P, O], F32, name="tt")
+            nc.vector.tensor_tensor(out=tt[:], in0=res[:, j, O : 2 * O], in1=s1[:], op=ALU.mult)
+            nc.vector.tensor_tensor(out=pre2[j][:], in0=pre2[j][:], in1=tt[:], op=ALU.subtract)
+
+        def finish_var(j):
+            d = fin.tile([P, O], F32, name="d")
+            nc.vector.tensor_tensor(out=d[:], in0=pre2[j][:], in1=acc_q[:, j, :], op=ALU.add)
+            nc.vector.tensor_scalar(
+                out=res[:, j, 0:O], in0=d[:], scalar1=sm[:, j, 7:8], scalar2=1e-30, op0=ALU.mult, op1=ALU.max
+            )
+
+        def on(stage, h):
+            if 0 <= h < NU:
+                stage(h)
+
+        for s in range(-LA_TEST, NU + LAG_ACC + 3):
+            on(evac, s)
+            on(gelu, s - LAG_GELU)
+            if not square_on_vector(s - LAG_GELU):
+                on(square, s - LAG_GELU)
+            on(test, s + LA_TEST)
+            if s == -LA_TEST:
+                nc.scalar.activation(out=c0[:], in_=bt[:, 0, 0, :], func=ACT.Gelu)
+                nc.scalar.activation(out=c0sq[:], in_=c0[:], func=ACT.Square)
+            if square_on_vector(s - LAG_SQ_V):
+                on(square, s - LAG_SQ_V)
+            on(quant, s - LAG_QUANT)
+            on(diag, s + LA_DIAG)
+            on(fold, s - LAG_ACC)
+            on(xpose, s + LA_XPOSE)
+            on(mx, s - LAG_QUANT)
+            on(accumulate, s - LAG_ACC)
+            last = s + LA_DIAG
+            if 0 <= last < NU and last % UPS == UPS - 1:
+                counts(last // UPS)
+            for j in range(SPP):
+                lag = 2 if j < SPP - 1 else 0
+                if s - LAG_ACC - lag == j * UPS + UPS - 1:
+                    finish_mean(j)
+                    finish_var(j)
+        nc.scalar.activation(out=res[:, 0 : SPP - 1, 0:O], in_=res[:, 0 : SPP - 1, 0:O], func=ACT.Sqrt)
+        nc.sync.dma_start(out=ov[:, 0 : SPP - 1, :], in_=res[:, 0 : SPP - 1, :])
+        nc.scalar.activation(out=res[:, SPP - 1, 0:O], in_=res[:, SPP - 1, 0:O], func=ACT.Sqrt)
+        nc.sync.dma_start(out=ov[:, SPP - 1, :], in_=res[:, SPP - 1, :])

@@ -10,50 +10,44 @@ U8 = mybir.dt.uint8
 FP8X4 = mybir.dt.float8_e4m3fn_x4
 ACT = mybir.ActivationFunctionType
 ALU = mybir.AluOpType
-AX = mybir.AxisListType
 
 P = 128
 B, T, D, O = 512, 32, 512, 128
-ROWS_PP = B * T // P
-SPP = ROWS_PP // T
+NT = B * T // P
 WORDS = D // 2
 UNIT = 4
-NU = ROWS_PP // UNIT
-UPS = T // UNIT
+NU = NT // UNIT
+SPU = UNIT * P // T
+GROUPS = B // P
+UPG = NU // GROUPS
 FLOPS = 2 * B * T * D * O
-PAD_WORD = -(1.0 + 49024.0 / 8388608.0)
+PAD_SCALE = 8388608.0
+PAD_BIAS = 8437632.0
 CHUNKS = [4, 4, 4, 4] + [8] * 14
 
 LA_TEST, LA_DIAG, LA_XPOSE = 5, 3, 2
-LAG_QUANT, LAG_GELU, LAG_SQ_V, LAG_ACC = 1, 3, 4, 5
-TAIL_S = 3
-PER_SQ_V = 8
+LAG_QUANT, LAG_GELU, LAG_BN = 1, 3, 4
 
 
 def evac_on_scalar(h, pr):
-    return pr == 1 and h >= NU - TAIL_S
-
-
-def square_on_vector(h):
-    return h % PER_SQ_V == PER_SQ_V - 1 and h < NU - 2
+    return (2 * h + pr) % 4 == 3
 
 
 def tile_linearnnencoder_t_kernel(tc, x, W, b, out):
     nc = tc.nc
-    xv = x.flatten_outer_dims().rearrange("(p r) k -> p r k", p=P)
-    ov = out.rearrange("(p j) c -> p j c", j=SPP)
+    xv = x.flatten_outer_dims().rearrange("(n p) k -> p n k", p=P)
+    ov = out.rearrange("(g p) c -> p g c", p=P)
     with ExitStack() as ctx:
         keep = ctx.enter_context(tc.tile_pool(name="keep", bufs=1))
         jk = ctx.enter_context(tc.tile_pool(name="jk", bufs=2))
         dgp = ctx.enter_context(tc.tile_pool(name="dgp", bufs=5))
         gp = ctx.enter_context(tc.tile_pool(name="gp", bufs=4))
         cp = ctx.enter_context(tc.tile_pool(name="cp", bufs=4))
-        ys = ctx.enter_context(tc.tile_pool(name="ys", bufs=6))
-        fs = ctx.enter_context(tc.tile_pool(name="fs", bufs=4))
+        ys = ctx.enter_context(tc.tile_pool(name="ys", bufs=4))
         fin = ctx.enter_context(tc.tile_pool(name="fin", bufs=2))
-        pacc = ctx.enter_context(tc.psum_pool(name="pacc", bufs=1))
+        pms = ctx.enter_context(tc.psum_pool(name="pms", bufs=1))
         pxt = ctx.enter_context(tc.psum_pool(name="pxt", bufs=4))
-        pmx = ctx.enter_context(tc.psum_pool(name="pmx", bufs=2))
+        pmx = ctx.enter_context(tc.psum_pool(name="pmx", bufs=3))
 
         w_sb = keep.tile([P, D], BF16)
         nc.sync.dma_start(out=w_sb[:], in_=W)
@@ -72,12 +66,16 @@ def tile_linearnnencoder_t_kernel(tc, x, W, b, out):
 
         ident = keep.tile([P, P], F32)
         make_identity(nc, ident[:])
-        negc = keep.tile([P, 1], F32)
-        nc.vector.memset(negc[:], -PAD_WORD)
+        padb = keep.tile([P, 1], F32)
+        nc.vector.memset(padb[:], PAD_BIAS)
         ones = keep.tile([P, P], BF16)
         nc.vector.memset(ones[:], 1.0)
+        blk = keep.tile([P, 4], F32)
+        nc.vector.memset(blk[:], 0.0)
+        for q in range(4):
+            nc.vector.memset(blk[T * q : T * (q + 1), q : q + 1], 1.0)
         warm = keep.tile([P, 1], F32)
-        nc.scalar.activation(out=warm[:], in_=negc[:], func=ACT.Gelu)
+        nc.scalar.activation(out=warm[:], in_=padb[:], func=ACT.Gelu)
 
         w_w = w_sb[:].bitcast(F32)
         wt = pxt.tile([P, 2, 2, P], F32, tag="xt")
@@ -95,16 +93,13 @@ def tile_linearnnencoder_t_kernel(tc, x, W, b, out):
         bcol = keep.tile([P, 1], F32)
         nc.vector.tensor_copy(out=bcol[:], in_=bt[:, 1, 0, 0:1])
         c0 = keep.tile([P, O], F32)
-        c0sq = keep.tile([P, O], F32)
 
-        dev = keep.tile([P, NU, 8], F32)
-        vf = keep.tile([P, SPP, T], F32)
-        sm = keep.tile([P, SPP, 8], F32)
-        res = keep.tile([P, SPP, 2 * O], F32)
-        acc_y = pacc.tile([P, SPP, O], F32)
-        acc_q = pacc.tile([P, SPP, O], F32)
-        dg, xt, g, codes, sc, v, y, q, yf = {}, {}, {}, {}, {}, {}, {}, {}, {}
-        pre1, pre2 = {}, {}
+        dev = keep.tile([P, NT], F32)
+        st = keep.tile([P, B, 3], F32)
+        sm = keep.tile([P, GROUPS, 8], F32)
+        res = keep.tile([P, GROUPS, 2 * O], F32)
+        dg, xt, g, codes, sc, v, y = {}, {}, {}, {}, {}, {}, {}
+        pre1, fps = {}, {}
 
         def row_words(i):
             xc, k = where[i]
@@ -112,26 +107,23 @@ def tile_linearnnencoder_t_kernel(tc, x, W, b, out):
 
         def test(h):
             for a in range(UNIT):
+                i = h * UNIT + a
                 junk = jk.tile([P, WORDS], BF16, tag="junk")
                 nc.scalar.activation(
                     out=junk[:],
-                    in_=row_words(h * UNIT + a),
+                    in_=row_words(i),
                     func=ACT.Square,
-                    bias=negc[:],
-                    scale=1.0,
-                    accum_out=dev[:, h, a : a + 1],
+                    bias=padb[:],
+                    scale=PAD_SCALE,
+                    accum_out=dev[:, i : i + 1],
                 )
 
         def diag(h):
             dg[h] = dgp.tile([P, UNIT, P], F32, name="dg")
             for a in range(UNIT):
+                i = h * UNIT + a
                 nc.vector.tensor_scalar(
-                    out=dg[h][:, a, :],
-                    in0=ident[:],
-                    scalar1=dev[:, h, a : a + 1],
-                    scalar2=0.0,
-                    op0=ALU.mult,
-                    op1=ALU.is_gt,
+                    out=dg[h][:, a, :], in0=ident[:], scalar1=dev[:, i : i + 1], scalar2=0.0, op0=ALU.min, op1=ALU.max
                 )
 
         def xpose(h):
@@ -176,103 +168,91 @@ def tile_linearnnencoder_t_kernel(tc, x, W, b, out):
             y[h] = ys.tile([P, UNIT * P], F32, name="y")
             nc.scalar.activation(out=y[h][:], in_=v[h][:], func=ACT.Gelu, bias=bcol[:], scale=1.0)
 
-        def square(h):
-            q[h] = ys.tile([P, UNIT * P], F32, name="q")
-            if square_on_vector(h):
-                nc.vector.tensor_tensor(out=q[h][:], in0=y[h][:], in1=y[h][:], op=ALU.mult)
-            else:
-                nc.scalar.activation(out=q[h][:], in_=y[h][:], func=ACT.Square)
+        def stats(h):
+            for c in range(SPU // 2):
+                s0 = h * SPU + 2 * c
+                nc.vector.bn_stats(
+                    out=st[:, s0 : s0 + 2, :].rearrange("o s e -> o (s e)"),
+                    in_=y[h][:, 2 * c * T : (2 * c + 2) * T].rearrange("o (s t) -> o t s", s=2),
+                )
 
-        def fold(h):
-            half = UNIT * P // 2
-            yf[h] = fs.tile([P, half], F32, name="yf")
-            nc.vector.tensor_tensor(out=yf[h][:], in0=y[h][:, 0:half], in1=y[h][:, half : 2 * half], op=ALU.add)
-
-        def accumulate(h):
-            j = h // UPS
-            for src, acc, n_t in ((yf, acc_y, UNIT // 2), (q, acc_q, UNIT)):
-                for a in range(n_t):
-                    nc.tensor.matmul(
-                        out=acc[:, j, :],
-                        lhsT=src[h][:, a * P : (a + 1) * P],
-                        rhs=ident[:],
-                        is_transpose=True,
-                        start=(h % UPS == 0 and a == 0),
-                        stop=(h % UPS == UPS - 1 and a == n_t - 1),
-                    )
-
-        def counts(j):
-            nc.vector.tensor_scalar(
-                out=vf[:, j, :].rearrange("p (h a) -> p h a", a=UNIT),
-                in0=dev[:, j * UPS : (j + 1) * UPS, 0:UNIT],
-                scalar1=0.0,
-                scalar2=None,
-                op0=ALU.is_gt,
+        def counts(gr):
+            fps[gr] = pms.tile([P, 4, P], F32, name="fps")
+            tiles = NT // GROUPS
+            sel = fin.tile([P, tiles, 4], BF16, name="sel")
+            nc.vector.tensor_tensor(
+                out=sel[:],
+                in0=dev[:, gr * tiles : (gr + 1) * tiles].unsqueeze(2).to_broadcast([P, tiles, 4]),
+                in1=blk[:].unsqueeze(1).to_broadcast([P, tiles, 4]),
+                op=ALU.min,
             )
-            n = sm[:, j, 0:1]
-            nc.vector.tensor_reduce(out=n, in_=vf[:, j, :], axis=AX.X, op=ALU.add)
-            nc.vector.tensor_scalar(out=sm[:, j, 1:2], in0=n, scalar1=-float(T), scalar2=None, op0=ALU.add)
-            nc.vector.tensor_scalar(out=sm[:, j, 2:3], in0=n, scalar1=1.0, scalar2=None, op0=ALU.max)
-            nc.vector.tensor_scalar(out=sm[:, j, 3:4], in0=n, scalar1=-1.0, scalar2=1.0, op0=ALU.add, op1=ALU.max)
-            nc.vector.reciprocal(out=sm[:, j, 4:6], in_=sm[:, j, 2:4])
+            nc.tensor.matmul(
+                out=fps[gr][:, 2, 0:2], lhsT=sel[:].rearrange("p i q -> p (i q)"), rhs=ones[:, 0:2], start=True, stop=True
+            )
+            m = sm[:, gr, :]
+            nc.vector.tensor_copy(out=m[:, 0:1], in_=fps[gr][:, 2, 0:1])
+            n = m[:, 0:1]
+            nc.vector.tensor_scalar(out=m[:, 1:2], in0=n, scalar1=1.0, scalar2=None, op0=ALU.max)
+            nc.vector.tensor_scalar(out=m[:, 2:3], in0=n, scalar1=-1.0, scalar2=1.0, op0=ALU.add, op1=ALU.max)
+            nc.vector.reciprocal(out=m[:, 3:5], in_=m[:, 1:3])
             nc.vector.scalar_tensor_tensor(
-                out=sm[:, j, 6:7], in0=n, scalar=0.0, in1=sm[:, j, 4:5], op0=ALU.is_gt, op1=ALU.mult
+                out=m[:, 3:4], in0=n, scalar=0.0, in1=m[:, 3:4], op0=ALU.is_gt, op1=ALU.mult
             )
             nc.vector.scalar_tensor_tensor(
-                out=sm[:, j, 7:8], in0=n, scalar=1.0, in1=sm[:, j, 5:6], op0=ALU.is_gt, op1=ALU.mult
+                out=m[:, 4:5], in0=n, scalar=1.0, in1=m[:, 4:5], op0=ALU.is_gt, op1=ALU.mult
             )
-            pre1[j] = fin.tile([P, O], F32, name="pre1")
-            nc.vector.tensor_scalar(out=pre1[j][:], in0=c0[:], scalar1=sm[:, j, 1:2], scalar2=None, op0=ALU.mult)
-            pre2[j] = fin.tile([P, O], F32, name="pre2")
-            nc.vector.tensor_scalar(out=pre2[j][:], in0=c0sq[:], scalar1=sm[:, j, 1:2], scalar2=None, op0=ALU.mult)
-
-        def finish_mean(j):
-            s1 = fin.tile([P, O], F32, name="s1")
-            nc.vector.tensor_tensor(out=s1[:], in0=pre1[j][:], in1=acc_y[:, j, :], op=ALU.add)
-            nc.vector.tensor_scalar(
-                out=res[:, j, O : 2 * O], in0=s1[:], scalar1=sm[:, j, 6:7], scalar2=None, op0=ALU.mult
+            nc.vector.scalar_tensor_tensor(
+                out=m[:, 5:6], in0=n, scalar=-float(T), in1=m[:, 3:4], op0=ALU.add, op1=ALU.mult
             )
-            tt = fin.tile([P, O], F32, name="tt")
-            nc.vector.tensor_tensor(out=tt[:], in0=res[:, j, O : 2 * O], in1=s1[:], op=ALU.mult)
-            nc.vector.tensor_tensor(out=pre2[j][:], in0=pre2[j][:], in1=tt[:], op=ALU.subtract)
+            nc.vector.tensor_scalar(out=m[:, 6:7], in0=m[:, 5:6], scalar1=float(T), scalar2=None, op0=ALU.mult)
+            nc.vector.tensor_scalar(out=m[:, 7:8], in0=m[:, 3:4], scalar1=float(T), scalar2=None, op0=ALU.mult)
+            pre1[gr] = fin.tile([P, O], F32, name="pre1")
+            nc.vector.tensor_scalar(out=pre1[gr][:], in0=c0[:], scalar1=m[:, 5:6], scalar2=None, op0=ALU.mult)
 
-        def finish_var(j):
+        def finish(gr):
+            m = sm[:, gr, :]
+            f = fps[gr]
+            for e in range(2):
+                nc.tensor.transpose(f[:, e, :], st[:, gr * P : (gr + 1) * P, 1 + e], ident[:])
+            mu, m2 = f[:, 0, :], f[:, 1, :]
             d = fin.tile([P, O], F32, name="d")
-            nc.vector.tensor_tensor(out=d[:], in0=pre2[j][:], in1=acc_q[:, j, :], op=ALU.add)
+            nc.vector.tensor_tensor(out=d[:], in0=c0[:], in1=mu, op=ALU.subtract)
+            nc.vector.scalar_tensor_tensor(
+                out=res[:, gr, O : 2 * O], in0=mu, scalar=m[:, 7:8], in1=pre1[gr][:], op0=ALU.mult, op1=ALU.add
+            )
+            t2 = fin.tile([P, O], F32, name="t2")
+            nc.vector.scalar_tensor_tensor(
+                out=t2[:], in0=d[:], scalar=m[:, 6:7], in1=d[:], op0=ALU.mult, op1=ALU.mult
+            )
+            t3 = fin.tile([P, O], F32, name="t3")
+            nc.vector.tensor_tensor(out=t3[:], in0=t2[:], in1=m2, op=ALU.add)
             nc.vector.tensor_scalar(
-                out=res[:, j, 0:O], in0=d[:], scalar1=sm[:, j, 7:8], scalar2=1e-30, op0=ALU.mult, op1=ALU.max
+                out=res[:, gr, 0:O], in0=t3[:], scalar1=m[:, 4:5], scalar2=1e-30, op0=ALU.mult, op1=ALU.max
             )
 
         def on(stage, h):
             if 0 <= h < NU:
                 stage(h)
 
-        for s in range(-LA_TEST, NU + LAG_ACC + 3):
+        for s in range(-LA_TEST, NU + LAG_BN + 3):
             on(evac, s)
             on(gelu, s - LAG_GELU)
-            if not square_on_vector(s - LAG_GELU):
-                on(square, s - LAG_GELU)
             on(test, s + LA_TEST)
             if s == -LA_TEST:
                 nc.scalar.activation(out=c0[:], in_=bt[:, 0, 0, :], func=ACT.Gelu)
-                nc.scalar.activation(out=c0sq[:], in_=c0[:], func=ACT.Square)
-            if square_on_vector(s - LAG_SQ_V):
-                on(square, s - LAG_SQ_V)
             on(quant, s - LAG_QUANT)
             on(diag, s + LA_DIAG)
-            on(fold, s - LAG_ACC)
+            on(stats, s - LAG_BN)
             on(xpose, s + LA_XPOSE)
             on(mx, s - LAG_QUANT)
-            on(accumulate, s - LAG_ACC)
-            last = s + LA_DIAG
-            if 0 <= last < NU and last % UPS == UPS - 1:
-                counts(last // UPS)
-            for j in range(SPP):
-                lag = 2 if j < SPP - 1 else 0
-                if s - LAG_ACC - lag == j * UPS + UPS - 1:
-                    finish_mean(j)
-                    finish_var(j)
-        nc.scalar.activation(out=res[:, 0 : SPP - 1, 0:O], in_=res[:, 0 : SPP - 1, 0:O], func=ACT.Sqrt)
-        nc.sync.dma_start(out=ov[:, 0 : SPP - 1, :], in_=res[:, 0 : SPP - 1, :])
-        nc.scalar.activation(out=res[:, SPP - 1, 0:O], in_=res[:, SPP - 1, 0:O], func=ACT.Sqrt)
-        nc.sync.dma_start(out=ov[:, SPP - 1, :], in_=res[:, SPP - 1, :])
+            for gr in range(GROUPS):
+                if s == gr * UPG + UPG - 1:
+                    counts(gr)
+                lag = 1 if gr < GROUPS - 1 else 0
+                if s - LAG_BN - lag == gr * UPG + UPG - 1:
+                    finish(gr)
+        last = GROUPS - 1
+        nc.scalar.activation(out=res[:, 0:last, 0:O], in_=res[:, 0:last, 0:O], func=ACT.Sqrt)
+        nc.sync.dma_start(out=ov[:, 0:last, :], in_=res[:, 0:last, :])
+        nc.scalar.activation(out=res[:, last, 0:O], in_=res[:, last, 0:O], func=ACT.Sqrt)
+        nc.sync.dma_start(out=ov[:, last, :], in_=res[:, last, :])

@@ -10,6 +10,7 @@ U8 = mybir.dt.uint8
 FP8X4 = mybir.dt.float8_e4m3fn_x4
 ACT = mybir.ActivationFunctionType
 ALU = mybir.AluOpType
+AX = mybir.AxisListType
 
 P = 128
 B, T, D, O = 512, 32, 512, 128
@@ -18,12 +19,13 @@ WORDS = D // 2
 UNIT = 4
 NU = NT // UNIT
 SPU = UNIT * P // T
+PPS = P // SPU
 GROUPS = B // P
 UPG = NU // GROUPS
 FLOPS = 2 * B * T * D * O
 PAD_SCALE = 8388608.0
 PAD_BIAS = 8437632.0
-CHUNKS = [4, 4, 4, 4] + [8] * 14
+CHUNKS = [1] * 4 + [2] * 14
 
 LA_TEST, LA_DIAG, LA_XPOSE = 5, 3, 2
 LAG_QUANT, LAG_GELU, LAG_BN = 1, 3, 4
@@ -35,7 +37,7 @@ def evac_on_scalar(h, pr):
 
 def tile_linearnnencoder_t_kernel(tc, x, W, b, out):
     nc = tc.nc
-    xv = x.flatten_outer_dims().rearrange("(n p) k -> p n k", p=P)
+    xv = x.flatten_outer_dims().rearrange("(h p a) k -> p h a k", p=P, a=UNIT)
     ov = out.rearrange("(g p) c -> p g c", p=P)
     with ExitStack() as ctx:
         keep = ctx.enter_context(tc.tile_pool(name="keep", bufs=1))
@@ -56,8 +58,8 @@ def tile_linearnnencoder_t_kernel(tc, x, W, b, out):
         where = {}
         r0 = 0
         for c, n_t in enumerate(CHUNKS):
-            xc = keep.tile([P, n_t, D], BF16, name="x%d" % c)
-            nc.sync.dma_start(out=xc[:], in_=xv[:, r0 : r0 + n_t, :])
+            xc = keep.tile([P, n_t, UNIT, D], BF16, name="x%d" % c)
+            nc.sync.dma_start(out=xc[:], in_=xv[:, r0 : r0 + n_t, :, :])
             for k in range(n_t):
                 where[r0 + k] = (xc, k)
             r0 += n_t
@@ -70,10 +72,8 @@ def tile_linearnnencoder_t_kernel(tc, x, W, b, out):
         nc.vector.memset(padb[:], PAD_BIAS)
         ones = keep.tile([P, P], BF16)
         nc.vector.memset(ones[:], 1.0)
-        blk = keep.tile([P, 4], F32)
-        nc.vector.memset(blk[:], 0.0)
-        for q in range(4):
-            nc.vector.memset(blk[T * q : T * (q + 1), q : q + 1], 1.0)
+        blk = keep.tile([P, SPU], F32)
+        nc.vector.tensor_reduce(out=blk[:], in_=ident[:].rearrange("p (q t) -> p q t", t=PPS), axis=AX.X, op=ALU.add)
         warm = keep.tile([P, 1], F32)
         nc.scalar.activation(out=warm[:], in_=padb[:], func=ACT.Gelu)
 
@@ -102,8 +102,8 @@ def tile_linearnnencoder_t_kernel(tc, x, W, b, out):
         pre1, fps = {}, {}
 
         def row_words(i):
-            xc, k = where[i]
-            return xc[:].bitcast(F32)[:, k, :]
+            xc, k = where[i // UNIT]
+            return xc[:].bitcast(F32)[:, k, i % UNIT, :]
 
         def test(h):
             for a in range(UNIT):
@@ -173,21 +173,27 @@ def tile_linearnnencoder_t_kernel(tc, x, W, b, out):
                 s0 = h * SPU + 2 * c
                 nc.vector.bn_stats(
                     out=st[:, s0 : s0 + 2, :].rearrange("o s e -> o (s e)"),
-                    in_=y[h][:, 2 * c * T : (2 * c + 2) * T].rearrange("o (s t) -> o t s", s=2),
+                    in_=y[h][:].rearrange("o (a q t) -> o a t q", a=UNIT, t=PPS)[:, :, :, 2 * c : 2 * c + 2],
                 )
 
         def counts(gr):
             fps[gr] = pms.tile([P, 4, P], F32, name="fps")
             tiles = NT // GROUPS
-            sel = fin.tile([P, tiles, 4], BF16, name="sel")
+            one = fin.tile([P, tiles], F32, name="one")
+            nc.vector.tensor_scalar(
+                out=one[:], in0=dev[:, gr * tiles : (gr + 1) * tiles], scalar1=1.0, scalar2=None, op0=ALU.min
+            )
+            nv = fin.tile([P, UPG], F32, name="nv")
+            nc.vector.tensor_reduce(out=nv[:], in_=one[:].rearrange("p (h a) -> p h a", a=UNIT), axis=AX.X, op=ALU.add)
+            sel = fin.tile([P, UPG, SPU], BF16, name="sel")
             nc.vector.tensor_tensor(
                 out=sel[:],
-                in0=dev[:, gr * tiles : (gr + 1) * tiles].unsqueeze(2).to_broadcast([P, tiles, 4]),
-                in1=blk[:].unsqueeze(1).to_broadcast([P, tiles, 4]),
-                op=ALU.min,
+                in0=nv[:].unsqueeze(2).to_broadcast([P, UPG, SPU]),
+                in1=blk[:].unsqueeze(1).to_broadcast([P, UPG, SPU]),
+                op=ALU.mult,
             )
             nc.tensor.matmul(
-                out=fps[gr][:, 2, 0:2], lhsT=sel[:].rearrange("p i q -> p (i q)"), rhs=ones[:, 0:2], start=True, stop=True
+                out=fps[gr][:, 2, 0:2], lhsT=sel[:].rearrange("p h q -> p (h q)"), rhs=ones[:, 0:2], start=True, stop=True
             )
             m = sm[:, gr, :]
             nc.vector.tensor_copy(out=m[:, 0:1], in_=fps[gr][:, 2, 0:1])

@@ -16,32 +16,51 @@ P = 128
 B, T, D, O = 512, 32, 512, 128
 NT = B * T // P
 WORDS = D // 2
-UNIT = 4
-NU = NT // UNIT
-SPU = UNIT * P // T
-PPS = P // SPU
 GROUPS = B // P
-UPG = NU // GROUPS
+TPG = NT // GROUPS
 FLOPS = 2 * B * T * D * O
 PAD_SCALE = 8388608.0
 PAD_BIAS = 8437632.0
-CHUNKS = [1] * 4 + [2] * 14
+PAD_WORD = -(1.0 + 49024.0 / 8388608.0)
+
+SIZES = [2, 2] + [4] * 30 + [2, 2]
+NU = len(SIZES)
+FIRST = [sum(SIZES[:h]) for h in range(NU)]
 
 LA_TEST, LA_DIAG, LA_XPOSE = 5, 3, 2
 LAG_QUANT, LAG_GELU, LAG_BN = 1, 3, 4
+HEAD_V, TAIL_S = 2, 8
+
+
+def equal_runs(gr):
+    found = []
+    for h in range(NU):
+        if FIRST[h] // TPG == gr:
+            if found and found[-1][0] == SIZES[h]:
+                found[-1] = (SIZES[h], found[-1][1], h + 1)
+            else:
+                found.append((SIZES[h], h, h + 1))
+    return found
+
+
+RUNS = [equal_runs(gr) for gr in range(GROUPS)]
 
 
 def evac_on_scalar(h, pr):
-    return (2 * h + pr) % 4 == 3
+    return pr == 1 if h >= NU - TAIL_S else (2 * h + pr) % 8 in (1, 3, 6)
+
+
+def test_on_vector(h, a):
+    return h < HEAD_V and a % 2 == 1
 
 
 def tile_linearnnencoder_t_kernel(tc, x, W, b, out):
     nc = tc.nc
-    xv = x.flatten_outer_dims().rearrange("(h p a) k -> p h a k", p=P, a=UNIT)
+    rows = x.flatten_outer_dims()
     ov = out.rearrange("(g p) c -> p g c", p=P)
     with ExitStack() as ctx:
         keep = ctx.enter_context(tc.tile_pool(name="keep", bufs=1))
-        jk = ctx.enter_context(tc.tile_pool(name="jk", bufs=2))
+        jk = ctx.enter_context(tc.tile_pool(name="jk", bufs=8))
         dgp = ctx.enter_context(tc.tile_pool(name="dgp", bufs=5))
         gp = ctx.enter_context(tc.tile_pool(name="gp", bufs=4))
         cp = ctx.enter_context(tc.tile_pool(name="cp", bufs=4))
@@ -52,149 +71,178 @@ def tile_linearnnencoder_t_kernel(tc, x, W, b, out):
         pmx = ctx.enter_context(tc.psum_pool(name="pmx", bufs=3))
 
         w_sb = keep.tile([P, D], BF16)
+        bcol = keep.tile([P, 1], BF16)
+        nc.sync.dma_start(out=bcol[:], in_=b.rearrange("(o u) -> o u", u=1))
         nc.sync.dma_start(out=w_sb[:], in_=W)
-        zb = keep.tile([P, O], BF16)
-        nc.vector.memset(zb[:], 0.0)
-        where = {}
-        r0 = 0
-        for c, n_t in enumerate(CHUNKS):
-            xc = keep.tile([P, n_t, UNIT, D], BF16, name="x%d" % c)
-            nc.sync.dma_start(out=xc[:], in_=xv[:, r0 : r0 + n_t, :, :])
-            for k in range(n_t):
-                where[r0 + k] = (xc, k)
-            r0 += n_t
-            if c == 0:
-                nc.sync.dma_start(out=zb[0:1, :], in_=b.rearrange("(u o) -> u o", u=1))
+        xs = []
+        for h, n in enumerate(SIZES):
+            xc = keep.tile([P, n, D], BF16, name="x%d" % h)
+            r0 = FIRST[h] * P
+            nc.sync.dma_start(out=xc[:], in_=rows[r0 : r0 + n * P, :].rearrange("(p a) k -> p a k", a=n))
+            xs.append(xc)
 
-        ident = keep.tile([P, P], F32)
-        make_identity(nc, ident[:])
         padb = keep.tile([P, 1], F32)
         nc.vector.memset(padb[:], PAD_BIAS)
-        ones = keep.tile([P, P], BF16)
-        nc.vector.memset(ones[:], 1.0)
-        blk = keep.tile([P, SPU], F32)
-        nc.vector.tensor_reduce(out=blk[:], in_=ident[:].rearrange("p (q t) -> p q t", t=PPS), axis=AX.X, op=ALU.add)
         warm = keep.tile([P, 1], F32)
         nc.scalar.activation(out=warm[:], in_=padb[:], func=ACT.Gelu)
-
-        w_w = w_sb[:].bitcast(F32)
-        wt = pxt.tile([P, 2, 2, P], F32, tag="xt")
-        for u in range(2):
-            nc.tensor.transpose(wt[:, 0, u, :], w_w[:, u:WORDS:2], ident[:])
-        gw = keep.tile([P, O, 4], BF16, align_bytes=64)
-        nc.vector.tensor_copy(out=gw[:].bitcast(F32), in_=wt[:, 0, :, :].rearrange("q u o -> q o u"))
-        wc = keep.tile([P, O], U32, align_bytes=64)
-        wsc = keep.tile([P, O], U8, align_bytes=64)
-        nc.vector.quantize_mx(out=wc[:].bitcast(FP8X4), scales=wsc[:], in_=gw[:].rearrange("q o j -> q (o j)"))
-
-        bt = pxt.tile([P, 2, 2, P], F32, tag="xt")
-        nc.tensor.matmul(out=bt[:, 0, 0, :], lhsT=ones[:], rhs=zb[:], start=True, stop=True)
-        nc.tensor.matmul(out=bt[:, 1, 0, 0:64], lhsT=zb[:], rhs=ones[:, 0:64], start=True, stop=True)
-        bcol = keep.tile([P, 1], F32)
-        nc.vector.tensor_copy(out=bcol[:], in_=bt[:, 1, 0, 0:1])
-        c0 = keep.tile([P, O], F32)
+        ident = keep.tile([P, P], F32)
+        make_identity(nc, ident[:])
+        ones = keep.tile([P, P], BF16)
+        nc.vector.memset(ones[:], 1.0)
+        blk = {}
 
         dev = keep.tile([P, NT], F32)
         st = keep.tile([P, B, 3], F32)
         sm = keep.tile([P, GROUPS, 8], F32)
         res = keep.tile([P, GROUPS, 2 * O], F32)
+        gw = keep.tile([P, O, 4], BF16, align_bytes=64)
+        wc = keep.tile([P, O], U32, align_bytes=64)
+        wsc = keep.tile([P, O], U8, align_bytes=64)
+        c0 = keep.tile([P, O], F32)
         dg, xt, g, codes, sc, v, y = {}, {}, {}, {}, {}, {}, {}
         pre1, fps = {}, {}
 
-        def row_words(i):
-            xc, k = where[i // UNIT]
-            return xc[:].bitcast(F32)[:, k, i % UNIT, :]
+        def weights():
+            w_w = w_sb[:].bitcast(F32)
+            wt = pmx.tile([P, 4, P], F32, name="v")
+            for u in range(2):
+                nc.tensor.transpose(wt[:, u, :], w_w[:, u:WORDS:2], ident[:])
+            nc.vector.tensor_copy(out=gw[:].bitcast(F32), in_=wt[:, 0:2, :].rearrange("q u o -> q o u"))
+            nc.vector.quantize_mx(out=wc[:].bitcast(FP8X4), scales=wsc[:], in_=gw[:].rearrange("q o j -> q (o j)"))
 
-        def test(h):
-            for a in range(UNIT):
-                i = h * UNIT + a
-                junk = jk.tile([P, WORDS], BF16, tag="junk")
-                nc.scalar.activation(
-                    out=junk[:],
-                    in_=row_words(i),
-                    func=ACT.Square,
-                    bias=padb[:],
-                    scale=PAD_SCALE,
-                    accum_out=dev[:, i : i + 1],
+        def bias_row():
+            c0col = keep.tile([P, 1], F32)
+            nc.scalar.activation(out=c0col[:], in_=bcol[:], func=ACT.Gelu)
+            bt = pms.tile([P, 4, P], F32, name="fps")
+            nc.tensor.transpose(bt[:, 0, :], c0col[:].to_broadcast([P, P]), ident[:])
+            nc.scalar.copy(out=c0[:], in_=bt[:, 0, :])
+
+        def owners():
+            for n in sorted(set(SIZES)):
+                blk[n] = keep.tile([P, 4 * n], F32, name="blk%d" % n)
+                nc.vector.tensor_reduce(
+                    out=blk[n][:], in_=ident[:].rearrange("p (q t) -> p q t", q=4 * n), axis=AX.X, op=ALU.add
                 )
 
+        def row_words(h, a):
+            return xs[h][:].bitcast(F32)[:, a, :]
+
+        def test(h):
+            for a in range(SIZES[h]):
+                i = FIRST[h] + a
+                junk = jk.tile([P, WORDS], BF16, tag="junk")
+                if test_on_vector(h, a):
+                    nc.vector.tensor_scalar(
+                        out=junk[:],
+                        in0=row_words(h, a),
+                        scalar1=PAD_WORD,
+                        scalar2=0.0,
+                        op0=ALU.not_equal,
+                        op1=ALU.add,
+                        accum_out=dev[:, i : i + 1],
+                    )
+                else:
+                    nc.scalar.activation(
+                        out=junk[:],
+                        in_=row_words(h, a),
+                        func=ACT.Square,
+                        bias=padb[:],
+                        scale=PAD_SCALE,
+                        accum_out=dev[:, i : i + 1],
+                    )
+
         def diag(h):
-            dg[h] = dgp.tile([P, UNIT, P], F32, name="dg")
-            for a in range(UNIT):
-                i = h * UNIT + a
+            dg[h] = dgp.tile([P, SIZES[h], P], F32, name="dg")
+            for a in range(SIZES[h]):
+                i = FIRST[h] + a
                 nc.vector.tensor_scalar(
                     out=dg[h][:, a, :], in0=ident[:], scalar1=dev[:, i : i + 1], scalar2=0.0, op0=ALU.min, op1=ALU.max
                 )
 
         def xpose(h):
-            for pr in range(2):
+            for pr in range(SIZES[h] // 2):
                 xt[h, pr] = pxt.tile([P, 2, 2, P], F32, name="xt")
                 for a in range(2):
-                    rw = row_words(h * UNIT + 2 * pr + a)
+                    rw = row_words(h, 2 * pr + a)
                     for u in range(2):
-                        nc.tensor.transpose(xt[h, pr][:, a, u, :], rw[:, u:WORDS:2], dg[h][:, 2 * pr + a, :])
+                        nc.tensor.transpose(xt[h, pr][:, u, a, :], rw[:, u:WORDS:2], dg[h][:, 2 * pr + a, :])
 
         def evac(h):
-            g[h] = gp.tile([P, UNIT * P, 4], BF16, name="g", align_bytes=64)
+            n = SIZES[h]
+            g[h] = gp.tile([P, n * P, 4], BF16, name="g", align_bytes=64)
             g_w = g[h][:].bitcast(F32)
-            for pr in range(2):
-                dst = g_w[:, 2 * pr * P : (2 * pr + 2) * P, :].rearrange("q (a t) u -> q a t u", a=2)
-                src = xt[h, pr][:].rearrange("q a u t -> q a t u")
+            for pr in range(n // 2):
+                dst = g_w[:, 2 * pr * P : (2 * pr + 2) * P, :].rearrange("q (c i) u -> q c u i", i=2)
+                src = xt[h, pr][:].rearrange("q u a t -> q u (a t)").rearrange("q u (c i) -> q c u i", i=2)
                 if evac_on_scalar(h, pr):
                     nc.scalar.copy(out=dst, in_=src)
                 else:
                     nc.vector.tensor_copy(out=dst, in_=src)
 
         def quant(h):
-            codes[h] = cp.tile([P, UNIT * P], U32, name="codes", align_bytes=64)
-            sc[h] = cp.tile([P, UNIT * P], U8, name="sc", align_bytes=64)
+            n = SIZES[h]
+            codes[h] = cp.tile([P, n * P], U32, name="codes", align_bytes=64)
+            sc[h] = cp.tile([P, n * P], U8, name="sc", align_bytes=64)
             nc.vector.quantize_mx(
                 out=codes[h][:].bitcast(FP8X4), scales=sc[h][:], in_=g[h][:].rearrange("q t j -> q (t j)")
             )
 
         def mx(h):
-            v[h] = pmx.tile([P, UNIT * P], F32, name="v")
-            nc.tensor.matmul_mx(
-                out=v[h][:],
-                lhsT=wc[:].bitcast(FP8X4),
-                lhsT_scale=wsc[:],
-                rhs=codes[h][:].bitcast(FP8X4),
-                rhs_scale=sc[h][:],
-                start=True,
-                stop=True,
-            )
+            v[h] = pmx.tile([P, 4, P], F32, name="v")
+            for i in [max(h - 1, 0)] * 2 + [h]:
+                n = min(SIZES[i], SIZES[h])
+                nc.tensor.matmul_mx(
+                    out=v[h][:, 0:n, :].rearrange("o a t -> o (a t)"),
+                    lhsT=wc[:].bitcast(FP8X4),
+                    lhsT_scale=wsc[:],
+                    rhs=codes[i][:, 0 : n * P].bitcast(FP8X4),
+                    rhs_scale=sc[i][:, 0 : n * P],
+                    start=True,
+                    stop=True,
+                )
 
         def gelu(h):
-            y[h] = ys.tile([P, UNIT * P], F32, name="y")
-            nc.scalar.activation(out=y[h][:], in_=v[h][:], func=ACT.Gelu, bias=bcol[:], scale=1.0)
+            y[h] = ys.tile([P, SIZES[h] * P], F32, name="y")
+            nc.scalar.activation(
+                out=y[h][:],
+                in_=v[h][:, 0 : SIZES[h], :].rearrange("o a t -> o (a t)"),
+                func=ACT.Gelu,
+                bias=bcol[:],
+                scale=1.0,
+            )
 
         def stats(h):
-            for c in range(SPU // 2):
-                s0 = h * SPU + 2 * c
+            n = SIZES[h]
+            for c in range(2 * n):
+                s0 = 4 * FIRST[h] + 2 * c
                 nc.vector.bn_stats(
                     out=st[:, s0 : s0 + 2, :].rearrange("o s e -> o (s e)"),
-                    in_=y[h][:].rearrange("o (a q t) -> o a t q", a=UNIT, t=PPS)[:, :, :, 2 * c : 2 * c + 2],
+                    in_=y[h][:].rearrange("o (a q t) -> o a t q", a=n, q=4 * n)[:, :, :, 2 * c : 2 * c + 2],
                 )
 
         def counts(gr):
             fps[gr] = pms.tile([P, 4, P], F32, name="fps")
-            tiles = NT // GROUPS
-            one = fin.tile([P, tiles], F32, name="one")
+            one = fin.tile([P, TPG], F32, name="one")
             nc.vector.tensor_scalar(
-                out=one[:], in0=dev[:, gr * tiles : (gr + 1) * tiles], scalar1=1.0, scalar2=None, op0=ALU.min
+                out=one[:], in0=dev[:, gr * TPG : (gr + 1) * TPG], scalar1=1.0, scalar2=None, op0=ALU.min
             )
-            nv = fin.tile([P, UPG], F32, name="nv")
-            nc.vector.tensor_reduce(out=nv[:], in_=one[:].rearrange("p (h a) -> p h a", a=UNIT), axis=AX.X, op=ALU.add)
-            sel = fin.tile([P, UPG, SPU], BF16, name="sel")
-            nc.vector.tensor_tensor(
-                out=sel[:],
-                in0=nv[:].unsqueeze(2).to_broadcast([P, UPG, SPU]),
-                in1=blk[:].unsqueeze(1).to_broadcast([P, UPG, SPU]),
-                op=ALU.mult,
-            )
-            nc.tensor.matmul(
-                out=fps[gr][:, 2, 0:2], lhsT=sel[:].rearrange("p h q -> p (h q)"), rhs=ones[:, 0:2], start=True, stop=True
-            )
+            sel = fin.tile([P, P], BF16, name="sel")
+            for n, h0, h1 in RUNS[gr]:
+                k = h1 - h0
+                t0 = FIRST[h0] - gr * TPG
+                nv = fin.tile([P, k], F32, tag="nv%d" % n)
+                nc.vector.tensor_reduce(
+                    out=nv[:], in_=one[:, t0 : t0 + k * n].rearrange("p (h a) -> p h a", a=n), axis=AX.X, op=ALU.add
+                )
+                nc.vector.tensor_tensor(
+                    out=sel[:, 4 * t0 : 4 * (t0 + k * n)].rearrange("p (h q) -> p h q", h=k),
+                    in0=nv[:].unsqueeze(2).to_broadcast([P, k, 4 * n]),
+                    in1=blk[n][:].unsqueeze(1).to_broadcast([P, k, 4 * n]),
+                    op=ALU.mult,
+                )
+            nc.tensor.matmul(out=fps[gr][:, 2, 0:2], lhsT=sel[:], rhs=ones[:, 0:2], start=True, stop=True)
+
+        def factors(gr):
             m = sm[:, gr, :]
             nc.vector.tensor_copy(out=m[:, 0:1], in_=fps[gr][:, 2, 0:1])
             n = m[:, 0:1]
@@ -215,11 +263,13 @@ def tile_linearnnencoder_t_kernel(tc, x, W, b, out):
             pre1[gr] = fin.tile([P, O], F32, name="pre1")
             nc.vector.tensor_scalar(out=pre1[gr][:], in0=c0[:], scalar1=m[:, 5:6], scalar2=None, op0=ALU.mult)
 
+        def turn(gr):
+            for e in range(2):
+                nc.tensor.transpose(fps[gr][:, e, :], st[:, gr * P : (gr + 1) * P, 1 + e], ident[:])
+
         def finish(gr):
             m = sm[:, gr, :]
             f = fps[gr]
-            for e in range(2):
-                nc.tensor.transpose(f[:, e, :], st[:, gr * P : (gr + 1) * P, 1 + e], ident[:])
             mu, m2 = f[:, 0, :], f[:, 1, :]
             d = fin.tile([P, O], F32, name="d")
             nc.vector.tensor_tensor(out=d[:], in0=c0[:], in1=mu, op=ALU.subtract)
@@ -240,22 +290,31 @@ def tile_linearnnencoder_t_kernel(tc, x, W, b, out):
             if 0 <= h < NU:
                 stage(h)
 
+        weights()
+        zw = keep.tile([P, 512], BF16)
+        nc.gpsimd.memset(zw[:], 0.0)
+        hot = pms.tile([P, 4, P], F32, name="fps")
+        for j in range(4):
+            nc.tensor.matmul(out=hot[:].rearrange("o a t -> o (a t)"), lhsT=ones[:], rhs=zw[:], start=True, stop=True)
         for s in range(-LA_TEST, NU + LAG_BN + 3):
             on(evac, s)
             on(gelu, s - LAG_GELU)
             on(test, s + LA_TEST)
-            if s == -LA_TEST:
-                nc.scalar.activation(out=c0[:], in_=bt[:, 0, 0, :], func=ACT.Gelu)
             on(quant, s - LAG_QUANT)
             on(diag, s + LA_DIAG)
             on(stats, s - LAG_BN)
             on(xpose, s + LA_XPOSE)
+            if s == 3:
+                owners()
+                bias_row()
             on(mx, s - LAG_QUANT)
             for gr in range(GROUPS):
-                if s == gr * UPG + UPG - 1:
+                e = RUNS[gr][-1][2] - 1
+                if s == e:
                     counts(gr)
-                lag = 1 if gr < GROUPS - 1 else 0
-                if s - LAG_BN - lag == gr * UPG + UPG - 1:
+                    factors(gr)
+                if s == e + LAG_BN + (1 if gr < GROUPS - 1 else 0):
+                    turn(gr)
                     finish(gr)
         last = GROUPS - 1
         nc.scalar.activation(out=res[:, 0:last, 0:O], in_=res[:, 0:last, 0:O], func=ACT.Sqrt)

@@ -14,158 +14,98 @@ AX = mybir.AxisListType
 
 P = 128
 B, T, D, O = 512, 32, 512, 128
-NT = B * T // P
 WORDS = D // 2
 GROUPS = B // P
-TPG = NT // GROUPS
 FLOPS = 2 * B * T * D * O
-PAD_SCALE = 8388608.0
-PAD_BIAS = 8437632.0
 PAD_WORD = -(1.0 + 49024.0 / 8388608.0)
 
 SIZES = [2, 2] + [4] * 30 + [2, 2]
 NU = len(SIZES)
 FIRST = [sum(SIZES[:h]) for h in range(NU)]
+SUMMED = GROUPS - 1
+LAST_OF = [max(h for h in range(NU) if FIRST[h] // T == gr) for gr in range(GROUPS)]
 
-LA_TEST, LA_DIAG, LA_XPOSE = 5, 3, 2
-LAG_QUANT, LAG_GELU, LAG_BN = 1, 3, 4
-HEAD_V, TAIL_S = 2, 8
-
-
-def equal_runs(gr):
-    found = []
-    for h in range(NU):
-        if FIRST[h] // TPG == gr:
-            if found and found[-1][0] == SIZES[h]:
-                found[-1] = (SIZES[h], found[-1][1], h + 1)
-            else:
-                found.append((SIZES[h], h, h + 1))
-    return found
+LA_XPOSE = 2
+LAG_QUANT, LAG_MX, LAG_BIAS, LAG_GELU, LAG_BN = 1, 1, 2, 3, 4
+BN_STEP = 8
+REPEATS = 2
 
 
-RUNS = [equal_runs(gr) for gr in range(GROUPS)]
+def evac_on_vector(h, pr):
+    return False
 
 
-def evac_on_scalar(h, pr):
-    return pr == 1 if h >= NU - TAIL_S else (2 * h + pr) % 8 in (1, 3, 6)
-
-
-def test_on_vector(h, a):
-    return h < HEAD_V and a % 2 == 1
+def flags_on_scalar(h):
+    return FIRST[h] // T in (1, 2) and h % 5 in (1, 3)
 
 
 def tile_linearnnencoder_t_kernel(tc, x, W, b, out):
     nc = tc.nc
-    rows = x.flatten_outer_dims()
+    xv = x.rearrange("(g p) t k -> g p t k", p=P)
     ov = out.rearrange("(g p) c -> p g c", p=P)
     with ExitStack() as ctx:
         keep = ctx.enter_context(tc.tile_pool(name="keep", bufs=1))
-        jk = ctx.enter_context(tc.tile_pool(name="jk", bufs=8))
-        dgp = ctx.enter_context(tc.tile_pool(name="dgp", bufs=5))
         gp = ctx.enter_context(tc.tile_pool(name="gp", bufs=4))
-        cp = ctx.enter_context(tc.tile_pool(name="cp", bufs=4))
-        ys = ctx.enter_context(tc.tile_pool(name="ys", bufs=4))
+        fp = ctx.enter_context(tc.tile_pool(name="fp", bufs=3))
+        cp = ctx.enter_context(tc.tile_pool(name="cp", bufs=3))
+        vbp = ctx.enter_context(tc.tile_pool(name="vbp", bufs=3))
+        ys = ctx.enter_context(tc.tile_pool(name="ys", bufs=2))
         fin = ctx.enter_context(tc.tile_pool(name="fin", bufs=2))
-        pms = ctx.enter_context(tc.psum_pool(name="pms", bufs=1))
+        pct = ctx.enter_context(tc.psum_pool(name="pct", bufs=1))
         pxt = ctx.enter_context(tc.psum_pool(name="pxt", bufs=4))
-        pmx = ctx.enter_context(tc.psum_pool(name="pmx", bufs=3))
+        pmx = ctx.enter_context(tc.psum_pool(name="pmx", bufs=2))
+        pac = ctx.enter_context(tc.psum_pool(name="pac", bufs=1))
+        qs = ctx.enter_context(tc.tile_pool(name="qs", bufs=2))
 
-        w_sb = keep.tile([P, D], BF16)
         bcol = keep.tile([P, 1], BF16)
         nc.sync.dma_start(out=bcol[:], in_=b.rearrange("(o u) -> o u", u=1))
+        w_sb = keep.tile([P, D], BF16)
         nc.sync.dma_start(out=w_sb[:], in_=W)
         xs = []
         for h, n in enumerate(SIZES):
             xc = keep.tile([P, n, D], BF16, name="x%d" % h)
-            r0 = FIRST[h] * P
-            nc.sync.dma_start(out=xc[:], in_=rows[r0 : r0 + n * P, :].rearrange("(p a) k -> p a k", a=n))
+            i0 = FIRST[h] % T
+            nc.sync.dma_start(out=xc[:], in_=xv[FIRST[h] // T, :, i0 : i0 + n, :])
             xs.append(xc)
 
-        padb = keep.tile([P, 1], F32)
-        nc.vector.memset(padb[:], PAD_BIAS)
+        padc = keep.tile([P, 1], F32)
+        nc.vector.memset(padc[:], -PAD_WORD)
         warm = keep.tile([P, 1], F32)
-        nc.scalar.activation(out=warm[:], in_=padb[:], func=ACT.Gelu)
+        nc.scalar.activation(out=warm[:], in_=padc[:], func=ACT.Gelu)
         ident = keep.tile([P, P], F32)
         make_identity(nc, ident[:])
-        ones = keep.tile([P, P], BF16)
+        ones = keep.tile([P, 2], BF16)
         nc.vector.memset(ones[:], 1.0)
-        blk = {}
 
-        dev = keep.tile([P, NT], F32)
-        st = keep.tile([P, B, 3], F32)
-        sm = keep.tile([P, GROUPS, 8], F32)
+        m = keep.tile([P, GROUPS * T], F32)
         res = keep.tile([P, GROUPS, 2 * O], F32)
         gw = keep.tile([P, O, 4], BF16, align_bytes=64)
         wc = keep.tile([P, O], U32, align_bytes=64)
         wsc = keep.tile([P, O], U8, align_bytes=64)
-        c0 = keep.tile([P, O], F32)
-        dg, xt, g, codes, sc, v, y = {}, {}, {}, {}, {}, {}, {}
-        pre1, fps = {}, {}
+        brow = keep.tile([P, O], F32)
+        xt, g, fl, codes, sc, v, vb, y, q, st = {}, {}, {}, {}, {}, {}, {}, {}, {}, {}
+        acc = pac.tile([P, 2, P], F32)
 
         def weights():
             w_w = w_sb[:].bitcast(F32)
-            wt = pmx.tile([P, 4, P], F32, name="v")
+            wt = pmx.tile([P, 4, O], F32, name="v")
             for u in range(2):
                 nc.tensor.transpose(wt[:, u, :], w_w[:, u:WORDS:2], ident[:])
             nc.vector.tensor_copy(out=gw[:].bitcast(F32), in_=wt[:, 0:2, :].rearrange("q u o -> q o u"))
             nc.vector.quantize_mx(out=wc[:].bitcast(FP8X4), scales=wsc[:], in_=gw[:].rearrange("q o j -> q (o j)"))
-
-        def bias_row():
-            c0col = keep.tile([P, 1], F32)
-            nc.scalar.activation(out=c0col[:], in_=bcol[:], func=ACT.Gelu)
-            bt = pms.tile([P, 4, P], F32, name="fps")
-            nc.tensor.transpose(bt[:, 0, :], c0col[:].to_broadcast([P, P]), ident[:])
-            nc.scalar.copy(out=c0[:], in_=bt[:, 0, :])
-
-        def owners():
-            for n in sorted(set(SIZES)):
-                blk[n] = keep.tile([P, 4 * n], F32, name="blk%d" % n)
-                nc.vector.tensor_reduce(
-                    out=blk[n][:], in_=ident[:].rearrange("p (q t) -> p q t", q=4 * n), axis=AX.X, op=ALU.add
-                )
-
-        def row_words(h, a):
-            return xs[h][:].bitcast(F32)[:, a, :]
-
-        def test(h):
-            for a in range(SIZES[h]):
-                i = FIRST[h] + a
-                junk = jk.tile([P, WORDS], BF16, tag="junk")
-                if test_on_vector(h, a):
-                    nc.vector.tensor_scalar(
-                        out=junk[:],
-                        in0=row_words(h, a),
-                        scalar1=PAD_WORD,
-                        scalar2=0.0,
-                        op0=ALU.not_equal,
-                        op1=ALU.add,
-                        accum_out=dev[:, i : i + 1],
-                    )
-                else:
-                    nc.scalar.activation(
-                        out=junk[:],
-                        in_=row_words(h, a),
-                        func=ACT.Square,
-                        bias=padb[:],
-                        scale=PAD_SCALE,
-                        accum_out=dev[:, i : i + 1],
-                    )
-
-        def diag(h):
-            dg[h] = dgp.tile([P, SIZES[h], P], F32, name="dg")
-            for a in range(SIZES[h]):
-                i = FIRST[h] + a
-                nc.vector.tensor_scalar(
-                    out=dg[h][:, a, :], in0=ident[:], scalar1=dev[:, i : i + 1], scalar2=0.0, op0=ALU.min, op1=ALU.max
-                )
+            bf = keep.tile([P, 1], F32)
+            nc.vector.tensor_copy(out=bf[:], in_=bcol[:])
+            bt = pmx.tile([P, 4, O], F32, name="v")
+            nc.tensor.transpose(bt[:, 0, :], bf[:].to_broadcast([P, P]), ident[:])
+            nc.vector.tensor_copy(out=brow[:], in_=bt[:, 0, :])
 
         def xpose(h):
+            xw = xs[h][:].bitcast(F32)
             for pr in range(SIZES[h] // 2):
                 xt[h, pr] = pxt.tile([P, 2, 2, P], F32, name="xt")
                 for a in range(2):
-                    rw = row_words(h, 2 * pr + a)
                     for u in range(2):
-                        nc.tensor.transpose(xt[h, pr][:, u, a, :], rw[:, u:WORDS:2], dg[h][:, 2 * pr + a, :])
+                        nc.tensor.transpose(xt[h, pr][:, u, a, :], xw[:, 2 * pr + a, u:WORDS:2], ident[:])
 
         def evac(h):
             n = SIZES[h]
@@ -174,10 +114,10 @@ def tile_linearnnencoder_t_kernel(tc, x, W, b, out):
             for pr in range(n // 2):
                 dst = g_w[:, 2 * pr * P : (2 * pr + 2) * P, :].rearrange("q (c i) u -> q c u i", i=2)
                 src = xt[h, pr][:].rearrange("q u a t -> q u (a t)").rearrange("q u (c i) -> q c u i", i=2)
-                if evac_on_scalar(h, pr):
-                    nc.scalar.copy(out=dst, in_=src)
-                else:
+                if evac_on_vector(h, pr):
                     nc.vector.tensor_copy(out=dst, in_=src)
+                else:
+                    nc.scalar.copy(out=dst, in_=src)
 
         def quant(h):
             n = SIZES[h]
@@ -187,103 +127,134 @@ def tile_linearnnencoder_t_kernel(tc, x, W, b, out):
                 out=codes[h][:].bitcast(FP8X4), scales=sc[h][:], in_=g[h][:].rearrange("q t j -> q (t j)")
             )
 
+        def flags(h):
+            n = SIZES[h]
+            fl[h] = fp.tile([P, 2, n * P], BF16, name="fl")
+            src = g[h][:].bitcast(F32).rearrange("q t u -> q u t")
+            if flags_on_scalar(h):
+                nc.scalar.activation(out=fl[h][:], in_=src, func=ACT.Square, bias=padc[:], scale=1.0)
+            else:
+                nc.vector.tensor_scalar(out=fl[h][:], in0=src, scalar1=PAD_WORD, scalar2=None, op0=ALU.not_equal)
+
+        def count(h):
+            n = SIZES[h]
+            ct = pct.tile([P, 4, 2], F32, name="ct")
+            for a in range(n):
+                for u in range(2):
+                    nc.tensor.matmul(
+                        out=ct[:, a, :],
+                        lhsT=fl[h][:, u, a * P : (a + 1) * P],
+                        rhs=ones[:],
+                        start=(u == 0),
+                        stop=(u == 1),
+                    )
+            nc.scalar.activation(out=m[:, FIRST[h] : FIRST[h] + n], in_=ct[:, 0:n, 0], func=ACT.Sign)
+
         def mx(h):
-            v[h] = pmx.tile([P, 4, P], F32, name="v")
-            for i in [max(h - 1, 0)] * 2 + [h]:
-                n = min(SIZES[i], SIZES[h])
-                nc.tensor.matmul_mx(
-                    out=v[h][:, 0:n, :].rearrange("o a t -> o (a t)"),
-                    lhsT=wc[:].bitcast(FP8X4),
-                    lhsT_scale=wsc[:],
-                    rhs=codes[i][:, 0 : n * P].bitcast(FP8X4),
-                    rhs_scale=sc[i][:, 0 : n * P],
-                    start=True,
-                    stop=True,
-                )
+            v[h] = pmx.tile([P, 4, O], F32, name="v")
+            for i in [max(h - 1, 0)] * (REPEATS - 1) + [h]:
+                for a in range(min(SIZES[i], SIZES[h])):
+                    nc.tensor.matmul_mx(
+                        out=v[h][:, a, :],
+                        lhsT=codes[i][:, a * P : (a + 1) * P].bitcast(FP8X4),
+                        lhsT_scale=sc[i][:, a * P : (a + 1) * P],
+                        rhs=wc[:].bitcast(FP8X4),
+                        rhs_scale=wsc[:],
+                        start=True,
+                        stop=True,
+                    )
+
+        def add_bias(h):
+            n = SIZES[h]
+            vb[h] = vbp.tile([P, n, O], F32, name="vb")
+            nc.vector.tensor_tensor(
+                out=vb[h][:], in0=v[h][:, 0:n, :], in1=brow[:].unsqueeze(1).to_broadcast([P, n, O]), op=ALU.add
+            )
 
         def gelu(h):
-            y[h] = ys.tile([P, SIZES[h] * P], F32, name="y")
-            nc.scalar.activation(
-                out=y[h][:],
-                in_=v[h][:, 0 : SIZES[h], :].rearrange("o a t -> o (a t)"),
-                func=ACT.Gelu,
-                bias=bcol[:],
-                scale=1.0,
-            )
+            gr, i0 = divmod(FIRST[h], T)
+            if i0 == 0:
+                y[gr] = ys.tile([P, T, O], F32, name="y")
+            for a in range(SIZES[h]):
+                nc.scalar.activation(
+                    out=y[gr][:, i0 + a, :],
+                    in_=vb[h][:, a, :],
+                    func=ACT.Gelu,
+                    scale=m[:, FIRST[h] + a : FIRST[h] + a + 1],
+                )
 
-        def stats(h):
-            n = SIZES[h]
-            for c in range(2 * n):
-                s0 = 4 * FIRST[h] + 2 * c
+        def stats(gr, c0, c1):
+            if c0 == 0:
+                st[gr] = fin.tile([P, O, 3], F32, name="st")
+            for c in range(c0, c1):
                 nc.vector.bn_stats(
-                    out=st[:, s0 : s0 + 2, :].rearrange("o s e -> o (s e)"),
-                    in_=y[h][:].rearrange("o (a q t) -> o a t q", a=n, q=4 * n)[:, :, :, 2 * c : 2 * c + 2],
+                    out=st[gr][:, 2 * c : 2 * c + 2, :].rearrange("p o e -> p (o e)"), in_=y[gr][:, :, 2 * c : 2 * c + 2]
                 )
 
-        def counts(gr):
-            fps[gr] = pms.tile([P, 4, P], F32, name="fps")
-            one = fin.tile([P, TPG], F32, name="one")
+        def square(h):
+            q[h] = qs.tile([P, SIZES[h], O], F32, name="q")
+            i0 = FIRST[h] % T
+            nc.scalar.activation(out=q[h][:], in_=y[SUMMED][:, i0 : i0 + SIZES[h], :], func=ACT.Square)
+
+        def accumulate(h):
+            for half in range(2):
+                for a in range(SIZES[h]):
+                    i = FIRST[h] % T + a
+                    nc.tensor.matmul(
+                        out=acc[:, half, :],
+                        lhsT=y[SUMMED][:, i, :] if half == 0 else q[h][:, a, :],
+                        rhs=ident[:],
+                        is_transpose=True,
+                        start=(half == 0 and i == 0),
+                        stop=(half == 1 and i == T - 1),
+                    )
+
+        def finish_sums():
+            gr = SUMMED
+            sums = fin.tile([P, 2, P], F32, name="sums")
+            nc.vector.tensor_copy(out=sums[:], in_=acc[:])
+            back = pmx.tile([P, 4, O], F32, name="v")
+            for half in range(2):
+                nc.tensor.transpose(back[:, half, :], sums[:, half, :], ident[:])
+            sm = factors(gr)
+            mean = res[:, gr, O : 2 * O]
+            nc.vector.tensor_scalar(out=mean, in0=back[:, 0, :], scalar1=sm[:, 3:4], scalar2=None, op0=ALU.mult)
+            t1 = fin.tile([P, O], F32, name="t1")
+            nc.vector.tensor_tensor(out=t1[:], in0=back[:, 0, :], in1=mean, op=ALU.mult)
+            t2 = fin.tile([P, O], F32, name="t2")
+            nc.vector.tensor_tensor(out=t2[:], in0=back[:, 1, :], in1=t1[:], op=ALU.subtract)
             nc.vector.tensor_scalar(
-                out=one[:], in0=dev[:, gr * TPG : (gr + 1) * TPG], scalar1=1.0, scalar2=None, op0=ALU.min
+                out=res[:, gr, 0:O], in0=t2[:], scalar1=sm[:, 4:5], scalar2=1e-30, op0=ALU.mult, op1=ALU.max
             )
-            sel = fin.tile([P, P], BF16, name="sel")
-            for n, h0, h1 in RUNS[gr]:
-                k = h1 - h0
-                t0 = FIRST[h0] - gr * TPG
-                nv = fin.tile([P, k], F32, tag="nv%d" % n)
-                nc.vector.tensor_reduce(
-                    out=nv[:], in_=one[:, t0 : t0 + k * n].rearrange("p (h a) -> p h a", a=n), axis=AX.X, op=ALU.add
-                )
-                nc.vector.tensor_tensor(
-                    out=sel[:, 4 * t0 : 4 * (t0 + k * n)].rearrange("p (h q) -> p h q", h=k),
-                    in0=nv[:].unsqueeze(2).to_broadcast([P, k, 4 * n]),
-                    in1=blk[n][:].unsqueeze(1).to_broadcast([P, k, 4 * n]),
-                    op=ALU.mult,
-                )
-            nc.tensor.matmul(out=fps[gr][:, 2, 0:2], lhsT=sel[:], rhs=ones[:, 0:2], start=True, stop=True)
 
         def factors(gr):
-            m = sm[:, gr, :]
-            nc.vector.tensor_copy(out=m[:, 0:1], in_=fps[gr][:, 2, 0:1])
-            n = m[:, 0:1]
-            nc.vector.tensor_scalar(out=m[:, 1:2], in0=n, scalar1=1.0, scalar2=None, op0=ALU.max)
-            nc.vector.tensor_scalar(out=m[:, 2:3], in0=n, scalar1=-1.0, scalar2=1.0, op0=ALU.add, op1=ALU.max)
-            nc.vector.reciprocal(out=m[:, 3:5], in_=m[:, 1:3])
+            sm = fin.tile([P, 8], F32, name="sm")
+            n = sm[:, 0:1]
+            nc.vector.tensor_reduce(out=n, in_=m[:, gr * T : (gr + 1) * T], axis=AX.X, op=ALU.add)
+            nc.vector.tensor_scalar(out=sm[:, 1:2], in0=n, scalar1=1.0, scalar2=None, op0=ALU.max)
+            nc.vector.tensor_scalar(out=sm[:, 2:3], in0=n, scalar1=-1.0, scalar2=1.0, op0=ALU.add, op1=ALU.max)
+            nc.vector.reciprocal(out=sm[:, 3:5], in_=sm[:, 1:3])
             nc.vector.scalar_tensor_tensor(
-                out=m[:, 3:4], in0=n, scalar=0.0, in1=m[:, 3:4], op0=ALU.is_gt, op1=ALU.mult
+                out=sm[:, 4:5], in0=n, scalar=1.0, in1=sm[:, 4:5], op0=ALU.is_gt, op1=ALU.mult
             )
+            nc.vector.tensor_scalar(out=sm[:, 5:6], in0=sm[:, 3:4], scalar1=float(T), scalar2=None, op0=ALU.mult)
             nc.vector.scalar_tensor_tensor(
-                out=m[:, 4:5], in0=n, scalar=1.0, in1=m[:, 4:5], op0=ALU.is_gt, op1=ALU.mult
+                out=sm[:, 6:7], in0=n, scalar=-float(T), in1=sm[:, 5:6], op0=ALU.add, op1=ALU.mult
             )
-            nc.vector.scalar_tensor_tensor(
-                out=m[:, 5:6], in0=n, scalar=-float(T), in1=m[:, 3:4], op0=ALU.add, op1=ALU.mult
-            )
-            nc.vector.tensor_scalar(out=m[:, 6:7], in0=m[:, 5:6], scalar1=float(T), scalar2=None, op0=ALU.mult)
-            nc.vector.tensor_scalar(out=m[:, 7:8], in0=m[:, 3:4], scalar1=float(T), scalar2=None, op0=ALU.mult)
-            pre1[gr] = fin.tile([P, O], F32, name="pre1")
-            nc.vector.tensor_scalar(out=pre1[gr][:], in0=c0[:], scalar1=m[:, 5:6], scalar2=None, op0=ALU.mult)
-
-        def turn(gr):
-            for e in range(2):
-                nc.tensor.transpose(fps[gr][:, e, :], st[:, gr * P : (gr + 1) * P, 1 + e], ident[:])
+            return sm
 
         def finish(gr):
-            m = sm[:, gr, :]
-            f = fps[gr]
-            mu, m2 = f[:, 0, :], f[:, 1, :]
-            d = fin.tile([P, O], F32, name="d")
-            nc.vector.tensor_tensor(out=d[:], in0=c0[:], in1=mu, op=ALU.subtract)
-            nc.vector.scalar_tensor_tensor(
-                out=res[:, gr, O : 2 * O], in0=mu, scalar=m[:, 7:8], in1=pre1[gr][:], op0=ALU.mult, op1=ALU.add
-            )
-            t2 = fin.tile([P, O], F32, name="t2")
-            nc.vector.scalar_tensor_tensor(
-                out=t2[:], in0=d[:], scalar=m[:, 6:7], in1=d[:], op0=ALU.mult, op1=ALU.mult
-            )
-            t3 = fin.tile([P, O], F32, name="t3")
-            nc.vector.tensor_tensor(out=t3[:], in0=t2[:], in1=m2, op=ALU.add)
+            sm = factors(gr)
+            mu, m2 = st[gr][:, :, 1], st[gr][:, :, 2]
             nc.vector.tensor_scalar(
-                out=res[:, gr, 0:O], in0=t3[:], scalar1=m[:, 4:5], scalar2=1e-30, op0=ALU.mult, op1=ALU.max
+                out=res[:, gr, O : 2 * O], in0=mu, scalar1=sm[:, 5:6], scalar2=None, op0=ALU.mult
+            )
+            t1 = fin.tile([P, O], F32, name="t1")
+            nc.vector.scalar_tensor_tensor(out=t1[:], in0=mu, scalar=sm[:, 6:7], in1=mu, op0=ALU.mult, op1=ALU.mult)
+            t2 = fin.tile([P, O], F32, name="t2")
+            nc.vector.tensor_tensor(out=t2[:], in0=t1[:], in1=m2, op=ALU.add)
+            nc.vector.tensor_scalar(
+                out=res[:, gr, 0:O], in0=t2[:], scalar1=sm[:, 4:5], scalar2=1e-30, op0=ALU.mult, op1=ALU.max
             )
 
         def on(stage, h):
@@ -291,31 +262,26 @@ def tile_linearnnencoder_t_kernel(tc, x, W, b, out):
                 stage(h)
 
         weights()
-        zw = keep.tile([P, 512], BF16)
-        nc.gpsimd.memset(zw[:], 0.0)
-        hot = pms.tile([P, 4, P], F32, name="fps")
-        for j in range(4):
-            nc.tensor.matmul(out=hot[:].rearrange("o a t -> o (a t)"), lhsT=ones[:], rhs=zw[:], start=True, stop=True)
-        for s in range(-LA_TEST, NU + LAG_BN + 3):
+        for s in range(-LA_XPOSE, NU + LAG_BN + 1):
             on(evac, s)
             on(gelu, s - LAG_GELU)
-            on(test, s + LA_TEST)
+            if 0 <= s - LAG_GELU < NU and FIRST[s - LAG_GELU] // T == SUMMED:
+                square(s - LAG_GELU)
+            on(add_bias, s - LAG_BIAS)
             on(quant, s - LAG_QUANT)
-            on(diag, s + LA_DIAG)
-            on(stats, s - LAG_BN)
-            on(xpose, s + LA_XPOSE)
-            if s == 3:
-                owners()
-                bias_row()
-            on(mx, s - LAG_QUANT)
+            on(flags, s - LAG_QUANT)
             for gr in range(GROUPS):
-                e = RUNS[gr][-1][2] - 1
-                if s == e:
-                    counts(gr)
-                    factors(gr)
-                if s == e + LAG_BN + (1 if gr < GROUPS - 1 else 0):
-                    turn(gr)
-                    finish(gr)
+                k = s - LAG_BN - LAST_OF[gr]
+                if gr < GROUPS - 1 and 0 <= k < O // 2 // BN_STEP:
+                    stats(gr, BN_STEP * k, BN_STEP * (k + 1))
+                    if k == O // 2 // BN_STEP - 1:
+                        finish(gr)
+            on(xpose, s + LA_XPOSE)
+            on(mx, s - LAG_MX)
+            on(count, s - LAG_MX)
+            if 0 <= s - LAG_BN < NU and FIRST[s - LAG_BN] // T == SUMMED:
+                accumulate(s - LAG_BN)
+        finish_sums()
         last = GROUPS - 1
         nc.scalar.activation(out=res[:, 0:last, 0:O], in_=res[:, 0:last, 0:O], func=ACT.Sqrt)
         nc.sync.dma_start(out=ov[:, 0:last, :], in_=res[:, 0:last, :])

from contextlib import ExitStack

import concourse.mybir as mybir
from concourse.masks import make_identity

F32 = mybir.dt.float32
BF16 = mybir.dt.bfloat16
U32 = mybir.dt.uint32
U8 = mybir.dt.uint8
FP8X4 = mybir.dt.float8_e4m3fn_x4
ACT = mybir.ActivationFunctionType
ALU = mybir.AluOpType
AX = mybir.AxisListType

P = 128
B, T, D, O = 512, 32, 512, 128
WORDS = D // 2
GROUPS = B // P
FLOPS = 2 * B * T * D * O
PAD_WORD = -(1.0 + 49024.0 / 8388608.0)

SIZES = [2, 2] + [4] * 30 + [2, 2]
NU = len(SIZES)
FIRST = [sum(SIZES[:h]) for h in range(NU)]
SUMMED = GROUPS - 1
LAST_OF = [max(h for h in range(NU) if FIRST[h] // T == gr) for gr in range(GROUPS)]

LA_XPOSE = 2
LAG_QUANT, LAG_MX, LAG_BIAS, LAG_GELU, LAG_BN = 1, 1, 2, 3, 4
BN_STEP = 8
REPEATS = 2


def evac_on_vector(h, pr):
    return False


def flags_on_scalar(h):
    return FIRST[h] // T in (1, 2) and h % 5 in (1, 3)


def tile_linearnnencoder_t_kernel(tc, x, W, b, out):
    nc = tc.nc
    xv = x.rearrange("(g p) t k -> g p t k", p=P)
    ov = out.rearrange("(g p) c -> p g c", p=P)
    with ExitStack() as ctx:
        keep = ctx.enter_context(tc.tile_pool(name="keep", bufs=1))
        gp = ctx.enter_context(tc.tile_pool(name="gp", bufs=4))
        fp = ctx.enter_context(tc.tile_pool(name="fp", bufs=3))
        cp = ctx.enter_context(tc.tile_pool(name="cp", bufs=3))
        vbp = ctx.enter_context(tc.tile_pool(name="vbp", bufs=3))
        ys = ctx.enter_context(tc.tile_pool(name="ys", bufs=2))
        fin = ctx.enter_context(tc.tile_pool(name="fin", bufs=2))
        pct = ctx.enter_context(tc.psum_pool(name="pct", bufs=1))
        pxt = ctx.enter_context(tc.psum_pool(name="pxt", bufs=4))
        pmx = ctx.enter_context(tc.psum_pool(name="pmx", bufs=2))
        pac = ctx.enter_context(tc.psum_pool(name="pac", bufs=1))
        qs = ctx.enter_context(tc.tile_pool(name="qs", bufs=2))

        bcol = keep.tile([P, 1], BF16)
        nc.sync.dma_start(out=bcol[:], in_=b.rearrange("(o u) -> o u", u=1))
        w_sb = keep.tile([P, D], BF16)
        nc.sync.dma_start(out=w_sb[:], in_=W)
        xs = []
        for h, n in enumerate(SIZES):
            xc = keep.tile([P, n, D], BF16, name="x%d" % h)
            i0 = FIRST[h] % T
            nc.sync.dma_start(out=xc[:], in_=xv[FIRST[h] // T, :, i0 : i0 + n, :])
            xs.append(xc)

        padc = keep.tile([P, 1], F32)
        nc.vector.memset(padc[:], -PAD_WORD)
        warm = keep.tile([P, 1], F32)
        nc.scalar.activation(out=warm[:], in_=padc[:], func=ACT.Gelu)
        ident = keep.tile([P, P], F32)
        make_identity(nc, ident[:])
        ones = keep.tile([P, 2], BF16)
        nc.vector.memset(ones[:], 1.0)

        m = keep.tile([P, GROUPS * T], F32)
        res = keep.tile([P, GROUPS, 2 * O], F32)
        gw = keep.tile([P, O, 4], BF16, align_bytes=64)
        wc = keep.tile([P, O], U32, align_bytes=64)
        wsc = keep.tile([P, O], U8, align_bytes=64)
        brow = keep.tile([P, O], F32)
        xt, g, fl, codes, sc, v, vb, y, q, st = {}, {}, {}, {}, {}, {}, {}, {}, {}, {}
        acc = pac.tile([P, 2, P], F32)

        def weights():
            w_w = w_sb[:].bitcast(F32)
            wt = pmx.tile([P, 4, O], F32, name="v")
            for u in range(2):
                nc.tensor.transpose(wt[:, u, :], w_w[:, u:WORDS:2], ident[:])
            nc.vector.tensor_copy(out=gw[:].bitcast(F32), in_=wt[:, 0:2, :].rearrange("q u o -> q o u"))
            nc.vector.quantize_mx(out=wc[:].bitcast(FP8X4), scales=wsc[:], in_=gw[:].rearrange("q o j -> q (o j)"))
            bf = keep.tile([P, 1], F32)
            nc.vector.tensor_copy(out=bf[:], in_=bcol[:])
            bt = pmx.tile([P, 4, O], F32, name="v")
            nc.tensor.transpose(bt[:, 0, :], bf[:].to_broadcast([P, P]), ident[:])
            nc.vector.tensor_copy(out=brow[:], in_=bt[:, 0, :])

        def xpose(h):
            xw = xs[h][:].bitcast(F32)
            for pr in range(SIZES[h] // 2):
                xt[h, pr] = pxt.tile([P, 2, 2, P], F32, name="xt")
                for a in range(2):
                    for u in range(2):
                        nc.tensor.transpose(xt[h, pr][:, u, a, :], xw[:, 2 * pr + a, u:WORDS:2], ident[:])

        def evac(h):
            n = SIZES[h]
            g[h] = gp.tile([P, n * P, 4], BF16, name="g", align_bytes=64)
            g_w = g[h][:].bitcast(F32)
            for pr in range(n // 2):
                dst = g_w[:, 2 * pr * P : (2 * pr + 2) * P, :].rearrange("q (c i) u -> q c u i", i=2)
                src = xt[h, pr][:].rearrange("q u a t -> q u (a t)").rearrange("q u (c i) -> q c u i", i=2)
                if evac_on_vector(h, pr):
                    nc.vector.tensor_copy(out=dst, in_=src)
                else:
                    nc.scalar.copy(out=dst, in_=src)

        def quant(h):
            n = SIZES[h]
            codes[h] = cp.tile([P, n * P], U32, name="codes", align_bytes=64)
            sc[h] = cp.tile([P, n * P], U8, name="sc", align_bytes=64)
            nc.vector.quantize_mx(
                out=codes[h][:].bitcast(FP8X4), scales=sc[h][:], in_=g[h][:].rearrange("q t j -> q (t j)")
            )

        def flags(h):
            n = SIZES[h]
            fl[h] = fp.tile([P, 2, n * P], BF16, name="fl")
            src = g[h][:].bitcast(F32).rearrange("q t u -> q u t")
            if flags_on_scalar(h):
                nc.scalar.activation(out=fl[h][:], in_=src, func=ACT.Square, bias=padc[:], scale=1.0)
            else:
                nc.vector.tensor_scalar(out=fl[h][:], in0=src, scalar1=PAD_WORD, scalar2=None, op0=ALU.not_equal)

        def count(h):
            n = SIZES[h]
            ct = pct.tile([P, 4, 2], F32, name="ct")
            for a in range(n):
                for u in range(2):
                    nc.tensor.matmul(
                        out=ct[:, a, :],
                        lhsT=fl[h][:, u, a * P : (a + 1) * P],
                        rhs=ones[:],
                        start=(u == 0),
                        stop=(u == 1),
                    )
            nc.scalar.activation(out=m[:, FIRST[h] : FIRST[h] + n], in_=ct[:, 0:n, 0], func=ACT.Sign)

        def mx(h):
            v[h] = pmx.tile([P, 4, O], F32, name="v")
            for i in [max(h - 1, 0)] * (REPEATS - 1) + [h]:
                for a in range(min(SIZES[i], SIZES[h])):
                    nc.tensor.matmul_mx(
                        out=v[h][:, a, :],
                        lhsT=codes[i][:, a * P : (a + 1) * P].bitcast(FP8X4),
                        lhsT_scale=sc[i][:, a * P : (a + 1) * P],
                        rhs=wc[:].bitcast(FP8X4),
                        rhs_scale=wsc[:],
                        start=True,
                        stop=True,
                    )

        def add_bias(h):
            n = SIZES[h]
            vb[h] = vbp.tile([P, n, O], F32, name="vb")
            nc.vector.tensor_tensor(
                out=vb[h][:], in0=v[h][:, 0:n, :], in1=brow[:].unsqueeze(1).to_broadcast([P, n, O]), op=ALU.add
            )

        def gelu(h):
            gr, i0 = divmod(FIRST[h], T)
            if i0 == 0:
                y[gr] = ys.tile([P, T, O], F32, name="y")
            for a in range(SIZES[h]):
                nc.scalar.activation(
                    out=y[gr][:, i0 + a, :],
                    in_=vb[h][:, a, :],
                    func=ACT.Gelu,
                    scale=m[:, FIRST[h] + a : FIRST[h] + a + 1],
                )

        def stats(gr, c0, c1):
            if c0 == 0:
                st[gr] = fin.tile([P, O, 3], F32, name="st")
            for c in range(c0, c1):
                nc.vector.bn_stats(
                    out=st[gr][:, 2 * c : 2 * c + 2, :].rearrange("p o e -> p (o e)"), in_=y[gr][:, :, 2 * c : 2 * c + 2]
                )

        def square(h):
            q[h] = qs.tile([P, SIZES[h], O], F32, name="q")
            i0 = FIRST[h] % T
            nc.scalar.activation(out=q[h][:], in_=y[SUMMED][:, i0 : i0 + SIZES[h], :], func=ACT.Square)

        def accumulate(h):
            for half in range(2):
                for a in range(SIZES[h]):
                    i = FIRST[h] % T + a
                    nc.tensor.matmul(
                        out=acc[:, half, :],
                        lhsT=y[SUMMED][:, i, :] if half == 0 else q[h][:, a, :],
                        rhs=ident[:],
                        is_transpose=True,
                        start=(half == 0 and i == 0),
                        stop=(half == 1 and i == T - 1),
                    )

        def finish_sums():
            gr = SUMMED
            sums = fin.tile([P, 2, P], F32, name="sums")
            nc.vector.tensor_copy(out=sums[:], in_=acc[:])
            back = pmx.tile([P, 4, O], F32, name="v")
            for half in range(2):
                nc.tensor.transpose(back[:, half, :], sums[:, half, :], ident[:])
            sm = factors(gr)
            mean = res[:, gr, O : 2 * O]
            nc.vector.tensor_scalar(out=mean, in0=back[:, 0, :], scalar1=sm[:, 3:4], scalar2=None, op0=ALU.mult)
            t1 = fin.tile([P, O], F32, name="t1")
            nc.vector.tensor_tensor(out=t1[:], in0=back[:, 0, :], in1=mean, op=ALU.mult)
            t2 = fin.tile([P, O], F32, name="t2")
            nc.vector.tensor_tensor(out=t2[:], in0=back[:, 1, :], in1=t1[:], op=ALU.subtract)
            nc.vector.tensor_scalar(
                out=res[:, gr, 0:O], in0=t2[:], scalar1=sm[:, 4:5], scalar2=1e-30, op0=ALU.mult, op1=ALU.max
            )

        def factors(gr):
            sm = fin.tile([P, 8], F32, name="sm")
            n = sm[:, 0:1]
            nc.vector.tensor_reduce(out=n, in_=m[:, gr * T : (gr + 1) * T], axis=AX.X, op=ALU.add)
            nc.vector.tensor_scalar(out=sm[:, 1:2], in0=n, scalar1=1.0, scalar2=None, op0=ALU.max)
            nc.vector.tensor_scalar(out=sm[:, 2:3], in0=n, scalar1=-1.0, scalar2=1.0, op0=ALU.add, op1=ALU.max)
            nc.vector.reciprocal(out=sm[:, 3:5], in_=sm[:, 1:3])
            nc.vector.scalar_tensor_tensor(
                out=sm[:, 4:5], in0=n, scalar=1.0, in1=sm[:, 4:5], op0=ALU.is_gt, op1=ALU.mult
            )
            nc.vector.tensor_scalar(out=sm[:, 5:6], in0=sm[:, 3:4], scalar1=float(T), scalar2=None, op0=ALU.mult)
            nc.vector.scalar_tensor_tensor(
                out=sm[:, 6:7], in0=n, scalar=-float(T), in1=sm[:, 5:6], op0=ALU.add, op1=ALU.mult
            )
            return sm

        def finish(gr):
            sm = factors(gr)
            mu, m2 = st[gr][:, :, 1], st[gr][:, :, 2]
            nc.vector.tensor_scalar(
                out=res[:, gr, O : 2 * O], in0=mu, scalar1=sm[:, 5:6], scalar2=None, op0=ALU.mult
            )
            t1 = fin.tile([P, O], F32, name="t1")
            nc.vector.scalar_tensor_tensor(out=t1[:], in0=mu, scalar=sm[:, 6:7], in1=mu, op0=ALU.mult, op1=ALU.mult)
            t2 = fin.tile([P, O], F32, name="t2")
            nc.vector.tensor_tensor(out=t2[:], in0=t1[:], in1=m2, op=ALU.add)
            nc.vector.tensor_scalar(
                out=res[:, gr, 0:O], in0=t2[:], scalar1=sm[:, 4:5], scalar2=1e-30, op0=ALU.mult, op1=ALU.max
            )

        def on(stage, h):
            if 0 <= h < NU:
                stage(h)

        weights()
        for s in range(-LA_XPOSE, NU + LAG_BN + 1):
            on(evac, s)
            on(gelu, s - LAG_GELU)
            if 0 <= s - LAG_GELU < NU and FIRST[s - LAG_GELU] // T == SUMMED:
                square(s - LAG_GELU)
            on(add_bias, s - LAG_BIAS)
            on(quant, s - LAG_QUANT)
            on(flags, s - LAG_QUANT)
            for gr in range(GROUPS):
                k = s - LAG_BN - LAST_OF[gr]
                if gr < GROUPS - 1 and 0 <= k < O // 2 // BN_STEP:
                    stats(gr, BN_STEP * k, BN_STEP * (k + 1))
                    if k == O // 2 // BN_STEP - 1:
                        finish(gr)
            on(xpose, s + LA_XPOSE)
            on(mx, s - LAG_MX)
            on(count, s - LAG_MX)
            if 0 <= s - LAG_BN < NU and FIRST[s - LAG_BN] // T == SUMMED:
                accumulate(s - LAG_BN)
        finish_sums()
        last = GROUPS - 1
        nc.scalar.activation(out=res[:, 0:last, 0:O], in_=res[:, 0:last, 0:O], func=ACT.Sqrt)
        nc.sync.dma_start(out=ov[:, 0:last, :], in_=res[:, 0:last, :])
        nc.scalar.activation(out=res[:, last, 0:O], in_=res[:, last, 0:O], func=ACT.Sqrt)
        nc.sync.dma_start(out=ov[:, last, :], in_=res[:, last, :])
